import numpy as np
import ml_dtypes


def mxq(x, axis, fmt="e4m3"):
    dtype, down = {"e4m3": (ml_dtypes.float8_e4m3fn, 7), "e5m2": (ml_dtypes.float8_e5m2, 14)}[fmt]
    v = np.moveaxis(np.asarray(x, np.float32).astype(ml_dtypes.bfloat16).astype(np.float64), axis, -1)
    blocks = v.reshape(v.shape[:-1] + (-1, 32))
    amax = np.abs(blocks).max(-1, keepdims=True)
    byte = np.maximum(np.where(amax > 0, np.frexp(amax)[1] - 1 + 127, 0) - down, 1)
    scale = np.exp2(byte - 127.0)
    codes = (blocks / scale).astype(np.float32).astype(dtype).astype(np.float64)
    return np.moveaxis((codes * scale).reshape(v.shape), -1, axis)


WIDE = False


def mx_kscale(k):
    if not WIDE:
        return np.ones(k)
    levels = np.array([10, -10, 5, -5, 0])
    a = np.random.permutation(np.resize(levels, k // 512 * 4)).reshape(k // 512, 4)
    idx = np.arange(k)
    return np.exp2(a[idx // 512, idx % 128 // 32])


BF16 = ml_dtypes.bfloat16


def bf(x):
    return np.asarray(x, np.float32).astype(BF16)


def f64(x):
    return np.asarray(x).astype(np.float64)


E2M1 = np.array([0.0, 0.5, 1.0, 1.5, 2.0, 3.0, 4.0, 6.0, -0.0, -0.5, -1.0, -1.5, -2.0, -3.0, -4.0, -6.0])


def pack_weight(w, fmt):
    k, n = w.shape
    w = f64(bf(w)).reshape(k // 32, 32, n)
    amax = np.abs(w).max(1)
    if fmt == "e4m3":
        byte = np.frexp(amax)[1] - 1 + 127 - 7
    else:
        mant, ex = np.frexp(amax / 6.0)
        byte = np.where(mant > 0.5, ex, ex - 1) + 127
    byte = np.clip(np.where(amax > 0, byte, 1), 1, 254)
    scaled = (w * np.exp2(127.0 - byte)[:, None, :]).reshape(k, n).astype(np.float32)
    by_word = np.ascontiguousarray(scaled.reshape(k // 512, 128, 4, n).transpose(0, 1, 3, 2))
    if fmt == "e4m3":
        words = by_word.astype(ml_dtypes.float8_e4m3fn).view(np.uint8)
    else:
        c = by_word.astype(ml_dtypes.float4_e2m1fn).view(np.uint8) & 0xF
        words = c[..., 0::2] | (c[..., 1::2] << 4)
    return np.ascontiguousarray(words), np.ascontiguousarray(byte.astype(np.uint8).reshape(k // 512, 16, n))


def unpack_weight(words, scales, fmt):
    g, p, n, _ = words.shape
    if fmt == "e4m3":
        vals = np.ascontiguousarray(words).view(ml_dtypes.float8_e4m3fn).astype(np.float64)
    else:
        nib = np.empty((g, p, n, 4), np.uint8)
        nib[..., 0::2] = words & 0xF
        nib[..., 1::2] = words >> 4
        vals = E2M1[nib]
    vals = vals * np.repeat(np.exp2(scales.astype(np.float64) - 127.0), 8, axis=1)[..., None]
    return vals.transpose(0, 1, 3, 2).reshape(g * 512, n)


B, NH, NW, C, K, P = 2, 16, 16, 1024, 256, 4
T = P * P
HAD = np.array([[1.0, 1.0, 1.0, 1.0],
                [1.0, -1.0, 1.0, -1.0],
                [1.0, 1.0, -1.0, -1.0],
                [1.0, -1.0, -1.0, 1.0]])


def setup_inputs():
    s = mx_kscale(C)
    trans = bf(np.random.standard_normal((T, B, NH, NW, C)) * s)
    weight = np.random.standard_normal((T, C, K)) * 0.5 * P / np.sqrt(C) / s[:, None]
    words, scales = pack_weight(weight.reshape(-1, K), "e4m3")
    bias = bf(np.random.standard_normal((1, 1, 1, K)) * 0.2)
    return {"trans": trans, "weight_words": words, "weight_scales": scales, "bias": bias}


def reference(trans, weight_words, weight_scales, bias):
    x = f64(trans).reshape(T, B * NH * NW, C)
    y = mxq(x, 2, "e4m3") @ unpack_weight(weight_words, weight_scales, "e4m3").reshape(T, C, K)
    y = y.reshape(P, P, B, NH, NW, K)
    r = np.stack([sum(HAD[p, u] * y[u] for u in range(P)) for p in range(P)])
    z = np.stack([sum(HAD[q, v] * r[:, v] for v in range(P)) for q in range(P)], axis=1) / T
    z = z.transpose(2, 3, 0, 4, 1, 5)
    return z.reshape(B, P * NH, P * NW, K) + f64(bias)

@@ -1,0 +1,220 @@
+from contextlib import ExitStack
+
+import concourse.mybir as mybir
+from concourse.masks import make_identity
+
+F32 = mybir.dt.float32
+BF16 = mybir.dt.bfloat16
+I32 = mybir.dt.int32
+U32 = mybir.dt.uint32
+U8 = mybir.dt.uint8
+FP8X4 = mybir.dt.float8_e4m3fn_x4
+ADD = mybir.AluOpType.add
+SUBTRACT = mybir.AluOpType.subtract
+MULT = mybir.AluOpType.mult
+COPY = mybir.ActivationFunctionType.Copy
+
+P = 128
+SIDE = 4
+C_IN = 1024
+C_OUT = 256
+K_PASS = 4 * P
+PASSES = C_IN // K_PASS
+ROW_TILES = 4
+PAIR = 2
+GROUPS = (ROW_TILES // PAIR) * SIDE
+STEPS = GROUPS * PAIR
+GROUPS_LOADED_AHEAD = 2
+PAIR_COLS = PAIR * SIDE * C_OUT
+
+FLOPS = 2 * SIDE * SIDE * ROW_TILES * P * C_IN * C_OUT
+
+
+def tile_iwht3layer_pa_t_e_kernel(tc, trans, weight_words, weight_scales, bias, out):
+    nc = tc.nc
+
+    x_dram = trans.rearrange("(u v) b i (jj rt) c -> u v (b i jj) (rt c)", v=SIDE, rt=ROW_TILES)
+    out_dram = out.rearrange("b (i p) (jj rt q) k -> p (b i) jj (rt q k)", p=SIDE, rt=ROW_TILES, q=SIDE)
+    w_dram = weight_words.rearrange("g p n t -> p g (n t)")
+
+    with ExitStack() as ctx:
+        const = ctx.enter_context(tc.tile_pool(name="const", bufs=1))
+        w_pool = ctx.enter_context(tc.tile_pool(name="w", bufs=SIDE))
+        x_pool = ctx.enter_context(tc.tile_pool(name="x", bufs=(GROUPS_LOADED_AHEAD + 1) * SIDE))
+        quant_pool = ctx.enter_context(tc.tile_pool(name="quant", bufs=3))
+        stage_pool = ctx.enter_context(tc.tile_pool(name="stage", bufs=2))
+        pixel_pool = ctx.enter_context(tc.tile_pool(name="pixel", bufs=4))
+        flip_psum = ctx.enter_context(tc.psum_pool(name="flip", bufs=SIDE))
+        y_psum = ctx.enter_context(tc.psum_pool(name="y", bufs=2))
+        ident = const.tile([P, P], F32)
+        make_identity(nc, ident[:])
+
+        bias_sb = const.tile([P, C_OUT], BF16)
+        nc.scalar.dma_start(out=bias_sb[:], in_=bias.rearrange("a b c k -> (a b c k)").partition_broadcast(P))
+
+        w_planes = const.tile([P, SIDE * SIDE * PASSES, C_OUT], U8, align_bytes=64)
+        nc.vector.memset(w_planes[:].bitcast(I32), 0)
+
+        ctx.enter_context(tc.manual_schedule())
+
+        x_tiles = {}
+        w_tiles = {}
+        grouped_tiles = {}
+        code_tiles = {}
+        odd_banks = {}
+        stage1_tiles = {}
+        stage2_tiles = {}
+        stage3_tiles = {}
+
+        def load_x(group):
+            half, u = divmod(group, SIDE)
+            x_tiles[group] = []
+            for v in range(SIDE):
+                x_raw = x_pool.tile([P, PAIR * C_IN], BF16)
+                nc.sync.dma_start(out=x_raw[:], in_=x_dram[u, v, :, half * PAIR * C_IN : (half + 1) * PAIR * C_IN])
+                x_tiles[group].append(x_raw)
+
+        def load_weight_scales():
+            for b in range(2):
+                for r in range(4):
+                    nc.sync.dma_start(
+                        out=w_planes[32 * b + r : P : 64, :, :].bitcast(I32),
+                        in_=weight_scales[:, 4 * b + r : 16 : 8, :].rearrange("g h n -> h g n").bitcast(I32),
+                    )
+
+        def load_weight_words(u):
+            w_words = w_pool.tile([P, SIDE * PASSES, C_OUT], U32, align_bytes=64)
+            first = u * SIDE * PASSES
+            nc.sync.dma_start(out=w_words[:].bitcast(I32), in_=w_dram[:, first : first + SIDE * PASSES, :].bitcast(I32))
+            w_tiles[u] = w_words
+
+        def transpose_and_regroup(step):
+            group, a = divmod(step, PAIR)
+            grouped = quant_pool.tile([P, SIDE * C_IN], BF16, align_bytes=64)
+            for v in range(SIDE):
+                x_words = x_tiles[group][v][:, a * C_IN : (a + 1) * C_IN].bitcast(F32)
+                flipped = flip_psum.tile([P, C_IN // 2], F32)
+                for g in range(PASSES):
+                    for w in range(2):
+                        nc.tensor.transpose(
+                            flipped[:, (2 * g + w) * P : (2 * g + w + 1) * P],
+                            x_words[:, (K_PASS // 2) * g + w : (K_PASS // 2) * (g + 1) : 2],
+                            ident[:],
+                        )
+                nc.scalar.copy(
+                    out=grouped[:, v * C_IN : (v + 1) * C_IN].bitcast(F32).rearrange("p (g r w) -> p g r w", g=PASSES, w=2),
+                    in_=flipped[:].rearrange("p (g w r) -> p g r w", g=PASSES, w=2),
+                )
+            grouped_tiles[step] = grouped
+
+        def quantise(step):
+            codes = quant_pool.tile([P, SIDE * PASSES * P], U32, align_bytes=64)
+            x_scales = quant_pool.tile([P, SIDE * PASSES * P], U8, align_bytes=64)
+            nc.vector.quantize_mx(out=codes[:].bitcast(FP8X4), scales=x_scales[:], in_=grouped_tiles[step][:])
+            code_tiles[step] = (codes, x_scales)
+
+        def multiply(step):
+            group, a = divmod(step, PAIR)
+            u = group % SIDE
+            codes, x_scales = code_tiles[step]
+
+            def mx_pass(acc, v, g, start, stop):
+                rows = slice((v * PASSES + g) * P, (v * PASSES + g + 1) * P)
+                nc.tensor.matmul_mx(
+                    out=acc,
+                    lhsT=codes[:, rows].bitcast(FP8X4),
+                    lhsT_scale=x_scales[:, rows],
+                    rhs=w_tiles[u][:, v * PASSES + g, :].bitcast(FP8X4),
+                    rhs_scale=w_planes[:, (u * SIDE + v) * PASSES + g, :],
+                    start=start,
+                    stop=stop,
+                )
+
+            sums = y_psum.tile([P, 2 * C_OUT], F32)
+            odds = y_psum.tile([P, 2 * C_OUT], F32)
+            for m in range(2):
+                cols = slice(m * C_OUT, (m + 1) * C_OUT)
+                for v in (2 * m, 2 * m + 1):
+                    for g in range(PASSES):
+                        mx_pass(sums[:, cols], v, g, start=(v == 2 * m and g == 0), stop=(v == 2 * m + 1 and g == PASSES - 1))
+                for g in range(PASSES):
+                    mx_pass(odds[:, cols], 2 * m + 1, g, start=(g == 0), stop=(g == PASSES - 1))
+            odd_banks[step] = odds
+
+            if a == 0:
+                stage1 = stage_pool.tile([P, PAIR, SIDE, C_OUT], F32)
+                stage1_tiles[group] = stage1
+            nc.scalar.activation(
+                out=stage1_tiles[group][:, a, 0:SIDE:2, :],
+                in_=sums[:].rearrange("p (m k) -> p m k", m=2),
+                func=COPY,
+                scale=1.0 / 16.0,
+            )
+
+        def butterfly(plus, minus, first, second):
+            nc.vector.tensor_tensor(out=plus, in0=first, in1=second, op=ADD)
+            nc.vector.tensor_tensor(out=minus, in0=first, in1=second, op=SUBTRACT)
+
+        def inverse_transform(step):
+            group, a = divmod(step, PAIR)
+            half, u = divmod(group, SIDE)
+            stage1 = stage1_tiles[group]
+            if u == 0:
+                nc.vector.tensor_tensor(out=stage1[:, a, 0, :], in0=stage1[:, a, 0, :], in1=bias_sb[:], op=ADD)
+            nc.vector.scalar_tensor_tensor(
+                out=stage1[:, a, 1:SIDE:2, :],
+                in0=odd_banks[step][:].rearrange("p (m k) -> p m k", m=2),
+                scalar=-2.0 / 16.0,
+                in1=stage1[:, a, 0:SIDE:2, :],
+                op0=MULT,
+                op1=ADD,
+            )
+            if a < PAIR - 1:
+                return
+
+            stage2 = stage_pool.tile([P, PAIR, SIDE, C_OUT], F32)
+            butterfly(stage2[:, :, 0:2, :], stage2[:, :, 2:4, :], stage1[:, :, 0:2, :], stage1[:, :, 2:4, :])
+            stage2_tiles[group] = stage2
+            if u % 2 == 0:
+                return
+
+            even_u = stage2_tiles[group - 1][:].rearrange("p a q k -> p (a q k)")
+            odd_u = stage2[:].rearrange("p a q k -> p (a q k)")
+            stage3_plus = stage_pool.tile([P, PAIR_COLS], F32)
+            stage3_minus = stage_pool.tile([P, PAIR_COLS], F32)
+            butterfly(stage3_plus[:], stage3_minus[:], even_u, odd_u)
+            stage3_tiles[(0, u // 2)] = stage3_plus
+            stage3_tiles[(1, u // 2)] = stage3_minus
+            if u < SIDE - 1:
+                return
+
+            for p in range(SIDE):
+                pixels = pixel_pool.tile([P, PAIR_COLS], F32)
+                nc.vector.tensor_tensor(
+                    out=pixels[:],
+                    in0=stage3_tiles[(p % 2, 0)][:],
+                    in1=stage3_tiles[(p % 2, 1)][:],
+                    op=(ADD if p < 2 else SUBTRACT),
+                )
+                nc.sync.dma_start(out=out_dram[p, :, :, half * PAIR_COLS : (half + 1) * PAIR_COLS], in_=pixels[:])
+
+        load_x(0)
+        load_weight_scales()
+        load_weight_words(0)
+        load_x(1)
+        load_weight_words(1)
+
+        for s in range(-1, STEPS + 1):
+            if s + 1 < STEPS:
+                group, a = divmod(s + 1, PAIR)
+                if a == 0 and group + GROUPS_LOADED_AHEAD < GROUPS:
+                    load_x(group + GROUPS_LOADED_AHEAD)
+                    if group + GROUPS_LOADED_AHEAD < SIDE:
+                        load_weight_words(group + GROUPS_LOADED_AHEAD)
+                transpose_and_regroup(s + 1)
+            if 0 <= s < STEPS:
+                multiply(s)
+            if s + 1 < STEPS:
+                quantise(s + 1)
+            if s >= 1:
+                inverse_transform(s - 1)

@@ -21,11 +21,9 @@ C_OUT = 256
 K_PASS = 4 * P
 PASSES = C_IN // K_PASS
 ROW_TILES = 4
-PAIR = 2
-GROUPS = (ROW_TILES // PAIR) * SIDE
-STEPS = GROUPS * PAIR
-GROUPS_LOADED_AHEAD = 2
-PAIR_COLS = PAIR * SIDE * C_OUT
+STEPS = ROW_TILES * SIDE
+STEPS_LOADED_AHEAD = 3
+ROW_COLS = SIDE * C_OUT
 
 FLOPS = 2 * SIDE * SIDE * ROW_TILES * P * C_IN * C_OUT
 
@@ -33,19 +31,20 @@ FLOPS = 2 * SIDE * SIDE * ROW_TILES * P * C_IN * C_OUT
 def tile_iwht3layer_pa_t_e_kernel(tc, trans, weight_words, weight_scales, bias, out):
     nc = tc.nc
 
-    x_dram = trans.rearrange("(u v) b i (jj rt) c -> u v (b i jj) (rt c)", v=SIDE, rt=ROW_TILES)
-    out_dram = out.rearrange("b (i p) (jj rt q) k -> p (b i) jj (rt q k)", p=SIDE, rt=ROW_TILES, q=SIDE)
+    x_dram = trans.rearrange("(u v) b i (jj rt) c -> u v rt (b i jj) c", v=SIDE, rt=ROW_TILES)
+    out_dram = out.rearrange("b (i p) (jj rt q) k -> p rt (b i) jj (q k)", p=SIDE, rt=ROW_TILES, q=SIDE)
     w_dram = weight_words.rearrange("g p n t -> p g (n t)")
 
     with ExitStack() as ctx:
         const = ctx.enter_context(tc.tile_pool(name="const", bufs=1))
         w_pool = ctx.enter_context(tc.tile_pool(name="w", bufs=SIDE))
-        x_pool = ctx.enter_context(tc.tile_pool(name="x", bufs=(GROUPS_LOADED_AHEAD + 1) * SIDE))
+        x_pool = ctx.enter_context(tc.tile_pool(name="x", bufs=(STEPS_LOADED_AHEAD + 1) * SIDE))
         quant_pool = ctx.enter_context(tc.tile_pool(name="quant", bufs=3))
-        stage_pool = ctx.enter_context(tc.tile_pool(name="stage", bufs=2))
-        pixel_pool = ctx.enter_context(tc.tile_pool(name="pixel", bufs=4))
+        stage_pool = ctx.enter_context(tc.tile_pool(name="stage", bufs=3))
+        pixel_pool = ctx.enter_context(tc.tile_pool(name="pixel", bufs=6))
         flip_psum = ctx.enter_context(tc.psum_pool(name="flip", bufs=SIDE))
         y_psum = ctx.enter_context(tc.psum_pool(name="y", bufs=2))
+
         ident = const.tile([P, P], F32)
         make_identity(nc, ident[:])
 
@@ -61,18 +60,18 @@ def tile_iwht3layer_pa_t_e_kernel(tc, trans, weight_words, weight_scales, bias, 
         w_tiles = {}
         grouped_tiles = {}
         code_tiles = {}
-        odd_banks = {}
+        y_banks = {}
         stage1_tiles = {}
         stage2_tiles = {}
         stage3_tiles = {}
 
-        def load_x(group):
-            half, u = divmod(group, SIDE)
-            x_tiles[group] = []
+        def load_x(step):
+            rt, u = divmod(step, SIDE)
+            x_tiles[step] = []
             for v in range(SIDE):
-                x_raw = x_pool.tile([P, PAIR * C_IN], BF16)
-                nc.sync.dma_start(out=x_raw[:], in_=x_dram[u, v, :, half * PAIR * C_IN : (half + 1) * PAIR * C_IN])
-                x_tiles[group].append(x_raw)
+                x_raw = x_pool.tile([P, C_IN], BF16)
+                nc.sync.dma_start(out=x_raw[:], in_=x_dram[u, v, rt])
+                x_tiles[step].append(x_raw)
 
         def load_weight_scales():
             for b in range(2):
@@ -88,11 +87,12 @@ def tile_iwht3layer_pa_t_e_kernel(tc, trans, weight_words, weight_scales, bias, 
             nc.sync.dma_start(out=w_words[:].bitcast(I32), in_=w_dram[:, first : first + SIDE * PASSES, :].bitcast(I32))
             w_tiles[u] = w_words
 
-        def transpose_and_regroup(step):
-            group, a = divmod(step, PAIR)
-            grouped = quant_pool.tile([P, SIDE * C_IN], BF16, align_bytes=64)
-            for v in range(SIDE):
-                x_words = x_tiles[group][v][:, a * C_IN : (a + 1) * C_IN].bitcast(F32)
+        def transpose_and_regroup(step, m):
+            if m == 0:
+                grouped = quant_pool.tile([P, SIDE * C_IN], BF16, align_bytes=64)
+                grouped_tiles[step] = grouped
+            for v in (2 * m, 2 * m + 1):
+                x_words = x_tiles[step][v][:].bitcast(F32)
                 flipped = flip_psum.tile([P, C_IN // 2], F32)
                 for g in range(PASSES):
                     for w in range(2):
@@ -102,10 +102,11 @@ def tile_iwht3layer_pa_t_e_kernel(tc, trans, weight_words, weight_scales, bias, 
                             ident[:],
                         )
                 nc.scalar.copy(
-                    out=grouped[:, v * C_IN : (v + 1) * C_IN].bitcast(F32).rearrange("p (g r w) -> p g r w", g=PASSES, w=2),
+                    out=grouped_tiles[step][:, v * C_IN : (v + 1) * C_IN]
+                    .bitcast(F32)
+                    .rearrange("p (g r w) -> p g r w", g=PASSES, w=2),
                     in_=flipped[:].rearrange("p (g w r) -> p g r w", g=PASSES, w=2),
                 )
-            grouped_tiles[step] = grouped
 
         def quantise(step):
             codes = quant_pool.tile([P, SIDE * PASSES * P], U32, align_bytes=64)
@@ -113,10 +114,14 @@ def tile_iwht3layer_pa_t_e_kernel(tc, trans, weight_words, weight_scales, bias, 
             nc.vector.quantize_mx(out=codes[:].bitcast(FP8X4), scales=x_scales[:], in_=grouped_tiles[step][:])
             code_tiles[step] = (codes, x_scales)
 
-        def multiply(step):
-            group, a = divmod(step, PAIR)
-            u = group % SIDE
+        def multiply(step, m):
+            u = step % SIDE
             codes, x_scales = code_tiles[step]
+            if m == 0:
+                sums = y_psum.tile([P, 2 * C_OUT], F32)
+                odds = y_psum.tile([P, 2 * C_OUT], F32)
+                y_banks[step] = (sums, odds)
+            sums, odds = y_banks[step]
 
             def mx_pass(acc, v, g, start, stop):
                 rows = slice((v * PASSES + g) * P, (v * PASSES + g + 1) * P)
@@ -130,91 +135,94 @@ def tile_iwht3layer_pa_t_e_kernel(tc, trans, weight_words, weight_scales, bias, 
                     stop=stop,
                 )
 
-            sums = y_psum.tile([P, 2 * C_OUT], F32)
-            odds = y_psum.tile([P, 2 * C_OUT], F32)
-            for m in range(2):
-                cols = slice(m * C_OUT, (m + 1) * C_OUT)
-                for v in (2 * m, 2 * m + 1):
-                    for g in range(PASSES):
-                        mx_pass(sums[:, cols], v, g, start=(v == 2 * m and g == 0), stop=(v == 2 * m + 1 and g == PASSES - 1))
+            cols = slice(m * C_OUT, (m + 1) * C_OUT)
+            for v in (2 * m, 2 * m + 1):
                 for g in range(PASSES):
-                    mx_pass(odds[:, cols], 2 * m + 1, g, start=(g == 0), stop=(g == PASSES - 1))
-            odd_banks[step] = odds
+                    mx_pass(sums[:, cols], v, g, start=(v == 2 * m and g == 0), stop=(v == 2 * m + 1 and g == PASSES - 1))
+            for g in range(PASSES):
+                mx_pass(odds[:, cols], 2 * m + 1, g, start=(g == 0), stop=(g == PASSES - 1))
 
-            if a == 0:
-                stage1 = stage_pool.tile([P, PAIR, SIDE, C_OUT], F32)
-                stage1_tiles[group] = stage1
+        def copy_sums(step):
+            stage1 = stage_pool.tile([P, SIDE, C_OUT], F32)
             nc.scalar.activation(
-                out=stage1_tiles[group][:, a, 0:SIDE:2, :],
-                in_=sums[:].rearrange("p (m k) -> p m k", m=2),
+                out=stage1[:, 0:SIDE:2, :],
+                in_=y_banks[step][0][:].rearrange("p (m k) -> p m k", m=2),
                 func=COPY,
                 scale=1.0 / 16.0,
+            )
+            stage1_tiles[step] = stage1
+
+        def differences(step):
+            stage1 = stage1_tiles[step]
+            if step % SIDE == 0:
+                nc.vector.tensor_tensor(out=stage1[:, 0, :], in0=stage1[:, 0, :], in1=bias_sb[:], op=ADD)
+            nc.vector.scalar_tensor_tensor(
+                out=stage1[:, 1:SIDE:2, :],
+                in0=y_banks[step][1][:].rearrange("p (m k) -> p m k", m=2),
+                scalar=-2.0 / 16.0,
+                in1=stage1[:, 0:SIDE:2, :],
+                op0=MULT,
+                op1=ADD,
             )
 
         def butterfly(plus, minus, first, second):
             nc.vector.tensor_tensor(out=plus, in0=first, in1=second, op=ADD)
             nc.vector.tensor_tensor(out=minus, in0=first, in1=second, op=SUBTRACT)
 
-        def inverse_transform(step):
-            group, a = divmod(step, PAIR)
-            half, u = divmod(group, SIDE)
-            stage1 = stage1_tiles[group]
-            if u == 0:
-                nc.vector.tensor_tensor(out=stage1[:, a, 0, :], in0=stage1[:, a, 0, :], in1=bias_sb[:], op=ADD)
-            nc.vector.scalar_tensor_tensor(
-                out=stage1[:, a, 1:SIDE:2, :],
-                in0=odd_banks[step][:].rearrange("p (m k) -> p m k", m=2),
-                scalar=-2.0 / 16.0,
-                in1=stage1[:, a, 0:SIDE:2, :],
-                op0=MULT,
-                op1=ADD,
-            )
-            if a < PAIR - 1:
-                return
-
-            stage2 = stage_pool.tile([P, PAIR, SIDE, C_OUT], F32)
-            butterfly(stage2[:, :, 0:2, :], stage2[:, :, 2:4, :], stage1[:, :, 0:2, :], stage1[:, :, 2:4, :])
-            stage2_tiles[group] = stage2
+        def later_butterflies(step):
+            rt, u = divmod(step, SIDE)
+            stage1 = stage1_tiles[step]
+            stage2 = stage_pool.tile([P, SIDE, C_OUT], F32)
+            butterfly(stage2[:, 0:2, :], stage2[:, 2:4, :], stage1[:, 0:2, :], stage1[:, 2:4, :])
+            stage2_tiles[step] = stage2
             if u % 2 == 0:
                 return
 
-            even_u = stage2_tiles[group - 1][:].rearrange("p a q k -> p (a q k)")
-            odd_u = stage2[:].rearrange("p a q k -> p (a q k)")
-            stage3_plus = stage_pool.tile([P, PAIR_COLS], F32)
-            stage3_minus = stage_pool.tile([P, PAIR_COLS], F32)
-            butterfly(stage3_plus[:], stage3_minus[:], even_u, odd_u)
+            stage3_plus = stage_pool.tile([P, ROW_COLS], F32)
+            stage3_minus = stage_pool.tile([P, ROW_COLS], F32)
+            butterfly(
+                stage3_plus[:],
+                stage3_minus[:],
+                stage2_tiles[step - 1][:].rearrange("p q k -> p (q k)"),
+                stage2[:].rearrange("p q k -> p (q k)"),
+            )
             stage3_tiles[(0, u // 2)] = stage3_plus
             stage3_tiles[(1, u // 2)] = stage3_minus
             if u < SIDE - 1:
                 return
 
             for p in range(SIDE):
-                pixels = pixel_pool.tile([P, PAIR_COLS], F32)
+                pixels = pixel_pool.tile([P, ROW_COLS], F32)
                 nc.vector.tensor_tensor(
                     out=pixels[:],
                     in0=stage3_tiles[(p % 2, 0)][:],
                     in1=stage3_tiles[(p % 2, 1)][:],
                     op=(ADD if p < 2 else SUBTRACT),
                 )
-                nc.sync.dma_start(out=out_dram[p, :, :, half * PAIR_COLS : (half + 1) * PAIR_COLS], in_=pixels[:])
+                nc.sync.dma_start(out=out_dram[p, rt], in_=pixels[:])
 
         load_x(0)
         load_weight_scales()
         load_weight_words(0)
-        load_x(1)
-        load_weight_words(1)
+        for step in range(1, STEPS_LOADED_AHEAD):
+            load_x(step)
+            load_weight_words(step)
 
         for s in range(-1, STEPS + 1):
-            if s + 1 < STEPS:
-                group, a = divmod(s + 1, PAIR)
-                if a == 0 and group + GROUPS_LOADED_AHEAD < GROUPS:
-                    load_x(group + GROUPS_LOADED_AHEAD)
-                    if group + GROUPS_LOADED_AHEAD < SIDE:
-                        load_weight_words(group + GROUPS_LOADED_AHEAD)
-                transpose_and_regroup(s + 1)
+            if s + STEPS_LOADED_AHEAD + 1 < STEPS:
+                load_x(s + STEPS_LOADED_AHEAD + 1)
+                if s + STEPS_LOADED_AHEAD + 1 < SIDE:
+                    load_weight_words(s + STEPS_LOADED_AHEAD + 1)
+            for m in range(2):
+                if s + 1 < STEPS:
+                    transpose_and_regroup(s + 1, m)
+                if 0 <= s < STEPS:
+                    multiply(s, m)
             if 0 <= s < STEPS:
-                multiply(s)
+                copy_sums(s)
+            if s >= 1:
+                differences(s - 1)
             if s + 1 < STEPS:
                 quantise(s + 1)
             if s >= 1:
-                inverse_transform(s - 1)
+                later_butterflies(s - 1)

@@ -213,12 +213,12 @@ def tile_iwht3layer_pa_t_e_kernel(tc, trans, weight_words, weight_scales, bias, 
                 load_x(s + STEPS_LOADED_AHEAD + 1)
                 if s + STEPS_LOADED_AHEAD + 1 < SIDE:
                     load_weight_words(s + STEPS_LOADED_AHEAD + 1)
-            for m in range(2):
-                if s + 1 < STEPS:
+            if s + 1 < STEPS:
+                for m in range(2):
                     transpose_and_regroup(s + 1, m)
-                if 0 <= s < STEPS:
-                    multiply(s, m)
             if 0 <= s < STEPS:
+                for m in range(2):
+                    multiply(s, m)
                 copy_sums(s)
             if s >= 1:
                 differences(s - 1)

@@ -214,12 +214,14 @@ def tile_iwht3layer_pa_t_e_kernel(tc, trans, weight_words, weight_scales, bias, 
                 if s + STEPS_LOADED_AHEAD + 1 < SIDE:
                     load_weight_words(s + STEPS_LOADED_AHEAD + 1)
             if s + 1 < STEPS:
-                for m in range(2):
-                    transpose_and_regroup(s + 1, m)
+                transpose_and_regroup(s + 1, 0)
+            if s >= 1:
+                multiply(s - 1, 1)
+                copy_sums(s - 1)
+            if s + 1 < STEPS:
+                transpose_and_regroup(s + 1, 1)
             if 0 <= s < STEPS:
-                for m in range(2):
-                    multiply(s, m)
-                copy_sums(s)
+                multiply(s, 0)
             if s >= 1:
                 differences(s - 1)
             if s + 1 < STEPS:

@@ -22,10 +22,17 @@ K_PASS = 4 * P
 PASSES = C_IN // K_PASS
 ROW_TILES = 4
 STEPS = ROW_TILES * SIDE
+STEPS_OF_A_HALF = STEPS // 2
 STEPS_LOADED_AHEAD = 3
 ROW_COLS = SIDE * C_OUT
 
 FLOPS = 2 * SIDE * SIDE * ROW_TILES * P * C_IN * C_OUT
+
+
+def place(step):
+    u_high, rest = divmod(step, STEPS_OF_A_HALF)
+    rt, u_low = divmod(rest, 2)
+    return rt, 2 * u_high + u_low
 
 
 def tile_iwht3layer_pa_t_e_kernel(tc, trans, weight_words, weight_scales, bias, out):
@@ -41,6 +48,7 @@ def tile_iwht3layer_pa_t_e_kernel(tc, trans, weight_words, weight_scales, bias, 
         x_pool = ctx.enter_context(tc.tile_pool(name="x", bufs=(STEPS_LOADED_AHEAD + 1) * SIDE))
         quant_pool = ctx.enter_context(tc.tile_pool(name="quant", bufs=3))
         stage_pool = ctx.enter_context(tc.tile_pool(name="stage", bufs=3))
+        stage3_pool = ctx.enter_context(tc.tile_pool(name="stage3", bufs=ROW_TILES + 2))
         pixel_pool = ctx.enter_context(tc.tile_pool(name="pixel", bufs=6))
         flip_psum = ctx.enter_context(tc.psum_pool(name="flip", bufs=SIDE))
         y_psum = ctx.enter_context(tc.psum_pool(name="y", bufs=2))
@@ -65,27 +73,30 @@ def tile_iwht3layer_pa_t_e_kernel(tc, trans, weight_words, weight_scales, bias, 
         stage2_tiles = {}
         stage3_tiles = {}
 
-        def load_x(step):
-            rt, u = divmod(step, SIDE)
-            x_tiles[step] = []
-            for v in range(SIDE):
-                x_raw = x_pool.tile([P, C_IN], BF16)
-                nc.sync.dma_start(out=x_raw[:], in_=x_dram[u, v, rt])
-                x_tiles[step].append(x_raw)
-
         def load_weight_scales():
-            for b in range(2):
-                for r in range(4):
-                    nc.sync.dma_start(
-                        out=w_planes[32 * b + r : P : 64, :, :].bitcast(I32),
-                        in_=weight_scales[:, 4 * b + r : 16 : 8, :].rearrange("g h n -> h g n").bitcast(I32),
-                    )
+            for r in range(4):
+                nc.sync.dma_start(
+                    out=w_planes[r : P : 32, :, :].bitcast(I32),
+                    in_=weight_scales[:, r : 16 : 4, :].rearrange("g q n -> q g n").bitcast(I32),
+                )
 
         def load_weight_words(u):
             w_words = w_pool.tile([P, SIDE * PASSES, C_OUT], U32, align_bytes=64)
             first = u * SIDE * PASSES
             nc.sync.dma_start(out=w_words[:].bitcast(I32), in_=w_dram[:, first : first + SIDE * PASSES, :].bitcast(I32))
             w_tiles[u] = w_words
+
+        def load_step(step):
+            rt, u = place(step)
+            x_tiles[step] = []
+            for v in range(SIDE):
+                x_raw = x_pool.tile([P, C_IN], BF16)
+                nc.sync.dma_start(out=x_raw[:], in_=x_dram[u, v, rt])
+                x_tiles[step].append(x_raw)
+            if step == 0:
+                load_weight_scales()
+            if rt == 0:
+                load_weight_words(u)
 
         def transpose_and_regroup(step, m):
             if m == 0:
@@ -115,7 +126,7 @@ def tile_iwht3layer_pa_t_e_kernel(tc, trans, weight_words, weight_scales, bias, 
             code_tiles[step] = (codes, x_scales)
 
         def multiply(step, m):
-            u = step % SIDE
+            u = place(step)[1]
             codes, x_scales = code_tiles[step]
             if m == 0:
                 sums = y_psum.tile([P, 2 * C_OUT], F32)
@@ -154,7 +165,7 @@ def tile_iwht3layer_pa_t_e_kernel(tc, trans, weight_words, weight_scales, bias, 
 
         def differences(step):
             stage1 = stage1_tiles[step]
-            if step % SIDE == 0:
+            if place(step)[1] == 0:
                 nc.vector.tensor_tensor(out=stage1[:, 0, :], in0=stage1[:, 0, :], in1=bias_sb[:], op=ADD)
             nc.vector.scalar_tensor_tensor(
                 out=stage1[:, 1:SIDE:2, :],
@@ -170,7 +181,7 @@ def tile_iwht3layer_pa_t_e_kernel(tc, trans, weight_words, weight_scales, bias, 
             nc.vector.tensor_tensor(out=minus, in0=first, in1=second, op=SUBTRACT)
 
         def later_butterflies(step):
-            rt, u = divmod(step, SIDE)
+            rt, u = place(step)
             stage1 = stage1_tiles[step]
             stage2 = stage_pool.tile([P, SIDE, C_OUT], F32)
             butterfly(stage2[:, 0:2, :], stage2[:, 2:4, :], stage1[:, 0:2, :], stage1[:, 2:4, :])
@@ -178,16 +189,16 @@ def tile_iwht3layer_pa_t_e_kernel(tc, trans, weight_words, weight_scales, bias, 
             if u % 2 == 0:
                 return
 
-            stage3_plus = stage_pool.tile([P, ROW_COLS], F32)
-            stage3_minus = stage_pool.tile([P, ROW_COLS], F32)
+            stage3_plus = stage3_pool.tile([P, ROW_COLS], F32)
+            stage3_minus = stage3_pool.tile([P, ROW_COLS], F32)
             butterfly(
                 stage3_plus[:],
                 stage3_minus[:],
                 stage2_tiles[step - 1][:].rearrange("p q k -> p (q k)"),
                 stage2[:].rearrange("p q k -> p (q k)"),
             )
-            stage3_tiles[(0, u // 2)] = stage3_plus
-            stage3_tiles[(1, u // 2)] = stage3_minus
+            stage3_tiles[(rt, 0, u // 2)] = stage3_plus
+            stage3_tiles[(rt, 1, u // 2)] = stage3_minus
             if u < SIDE - 1:
                 return
 
@@ -195,33 +206,25 @@ def tile_iwht3layer_pa_t_e_kernel(tc, trans, weight_words, weight_scales, bias, 
                 pixels = pixel_pool.tile([P, ROW_COLS], F32)
                 nc.vector.tensor_tensor(
                     out=pixels[:],
-                    in0=stage3_tiles[(p % 2, 0)][:],
-                    in1=stage3_tiles[(p % 2, 1)][:],
+                    in0=stage3_tiles[(rt, p % 2, 0)][:],
+                    in1=stage3_tiles[(rt, p % 2, 1)][:],
                     op=(ADD if p < 2 else SUBTRACT),
                 )
                 nc.sync.dma_start(out=out_dram[p, rt], in_=pixels[:])
 
-        load_x(0)
-        load_weight_scales()
-        load_weight_words(0)
-        for step in range(1, STEPS_LOADED_AHEAD):
-            load_x(step)
-            load_weight_words(step)
+        for step in range(STEPS_LOADED_AHEAD):
+            load_step(step)
 
         for s in range(-1, STEPS + 1):
             if s + STEPS_LOADED_AHEAD + 1 < STEPS:
-                load_x(s + STEPS_LOADED_AHEAD + 1)
-                if s + STEPS_LOADED_AHEAD + 1 < SIDE:
-                    load_weight_words(s + STEPS_LOADED_AHEAD + 1)
+                load_step(s + STEPS_LOADED_AHEAD + 1)
             if s + 1 < STEPS:
-                transpose_and_regroup(s + 1, 0)
-            if s >= 1:
-                multiply(s - 1, 1)
-                copy_sums(s - 1)
-            if s + 1 < STEPS:
-                transpose_and_regroup(s + 1, 1)
+                for m in range(2):
+                    transpose_and_regroup(s + 1, m)
             if 0 <= s < STEPS:
-                multiply(s, 0)
+                for m in range(2):
+                    multiply(s, m)
+                copy_sums(s)
             if s >= 1:
                 differences(s - 1)
             if s + 1 < STEPS:

@@ -47,7 +47,7 @@ def tile_iwht3layer_pa_t_e_kernel(tc, trans, weight_words, weight_scales, bias, 
         w_pool = ctx.enter_context(tc.tile_pool(name="w", bufs=SIDE))
         x_pool = ctx.enter_context(tc.tile_pool(name="x", bufs=(STEPS_LOADED_AHEAD + 1) * SIDE))
         quant_pool = ctx.enter_context(tc.tile_pool(name="quant", bufs=3))
-        stage_pool = ctx.enter_context(tc.tile_pool(name="stage", bufs=3))
+        stage_pool = ctx.enter_context(tc.tile_pool(name="stage", bufs=5))
         stage3_pool = ctx.enter_context(tc.tile_pool(name="stage3", bufs=ROW_TILES + 2))
         pixel_pool = ctx.enter_context(tc.tile_pool(name="pixel", bufs=6))
         flip_psum = ctx.enter_context(tc.psum_pool(name="flip", bufs=SIDE))
@@ -125,14 +125,12 @@ def tile_iwht3layer_pa_t_e_kernel(tc, trans, weight_words, weight_scales, bias, 
             nc.vector.quantize_mx(out=codes[:].bitcast(FP8X4), scales=x_scales[:], in_=grouped_tiles[step][:])
             code_tiles[step] = (codes, x_scales)
 
-        def multiply(step, m):
+        def multiply(step):
             u = place(step)[1]
             codes, x_scales = code_tiles[step]
-            if m == 0:
-                sums = y_psum.tile([P, 2 * C_OUT], F32)
-                odds = y_psum.tile([P, 2 * C_OUT], F32)
-                y_banks[step] = (sums, odds)
-            sums, odds = y_banks[step]
+            bank_a = y_psum.tile([P, 2 * C_OUT], F32)
+            bank_b = y_psum.tile([P, 2 * C_OUT], F32)
+            y_banks[step] = (bank_a, bank_b)
 
             def mx_pass(acc, v, g, start, stop):
                 rows = slice((v * PASSES + g) * P, (v * PASSES + g + 1) * P)
@@ -146,32 +144,37 @@ def tile_iwht3layer_pa_t_e_kernel(tc, trans, weight_words, weight_scales, bias, 
                     stop=stop,
                 )
 
-            cols = slice(m * C_OUT, (m + 1) * C_OUT)
-            for v in (2 * m, 2 * m + 1):
-                for g in range(PASSES):
-                    mx_pass(sums[:, cols], v, g, start=(v == 2 * m and g == 0), stop=(v == 2 * m + 1 and g == PASSES - 1))
-            for g in range(PASSES):
-                mx_pass(odds[:, cols], 2 * m + 1, g, start=(g == 0), stop=(g == PASSES - 1))
+            for acc, members in (
+                (bank_b[:, 0:C_OUT], (2, 3)),
+                (bank_b[:, C_OUT : 2 * C_OUT], (1, 2)),
+                (bank_a[:, 0:C_OUT], (1, 3)),
+                (bank_a[:, C_OUT : 2 * C_OUT], (0, 1, 2, 3)),
+            ):
+                for v in members:
+                    for g in range(PASSES):
+                        mx_pass(acc, v, g, start=(v == members[0] and g == 0), stop=(v == members[-1] and g == PASSES - 1))
 
         def copy_sums(step):
-            stage1 = stage_pool.tile([P, SIDE, C_OUT], F32)
-            nc.scalar.activation(
-                out=stage1[:, 0:SIDE:2, :],
-                in_=y_banks[step][0][:].rearrange("p (m k) -> p m k", m=2),
-                func=COPY,
-                scale=1.0 / 16.0,
-            )
-            stage1_tiles[step] = stage1
+            stage2 = stage_pool.tile([P, SIDE, C_OUT], F32)
+            stage2_tiles[step] = stage2
+            if place(step)[1] != 0:
+                nc.scalar.activation(out=stage2[:, 0, :], in_=y_banks[step][0][:, C_OUT : 2 * C_OUT], func=COPY, scale=1.0 / 16.0)
 
         def differences(step):
-            stage1 = stage1_tiles[step]
+            stage2 = stage2_tiles[step]
+            bank_a, bank_b = y_banks[step]
             if place(step)[1] == 0:
-                nc.vector.tensor_tensor(out=stage1[:, 0, :], in0=stage1[:, 0, :], in1=bias_sb[:], op=ADD)
+                nc.vector.scalar_tensor_tensor(
+                    out=stage2[:, 0, :], in0=bank_a[:, C_OUT : 2 * C_OUT], scalar=1.0 / 16.0, in1=bias_sb[:], op0=MULT, op1=ADD
+                )
             nc.vector.scalar_tensor_tensor(
-                out=stage1[:, 1:SIDE:2, :],
-                in0=y_banks[step][1][:].rearrange("p (m k) -> p m k", m=2),
+                out=stage2[:, 1, :], in0=bank_a[:, 0:C_OUT], scalar=-2.0 / 16.0, in1=stage2[:, 0, :], op0=MULT, op1=ADD
+            )
+            nc.vector.scalar_tensor_tensor(
+                out=stage2[:, 2:4, :],
+                in0=bank_b[:].rearrange("p (m k) -> p m k", m=2),
                 scalar=-2.0 / 16.0,
-                in1=stage1[:, 0:SIDE:2, :],
+                in1=stage2[:, 0:1, :].to_broadcast([P, 2, C_OUT]),
                 op0=MULT,
                 op1=ADD,
             )
@@ -182,10 +185,7 @@ def tile_iwht3layer_pa_t_e_kernel(tc, trans, weight_words, weight_scales, bias, 
 
         def later_butterflies(step):
             rt, u = place(step)
-            stage1 = stage1_tiles[step]
-            stage2 = stage_pool.tile([P, SIDE, C_OUT], F32)
-            butterfly(stage2[:, 0:2, :], stage2[:, 2:4, :], stage1[:, 0:2, :], stage1[:, 2:4, :])
-            stage2_tiles[step] = stage2
+            stage2 = stage2_tiles[step]
             if u % 2 == 0:
                 return
 
@@ -222,8 +222,7 @@ def tile_iwht3layer_pa_t_e_kernel(tc, trans, weight_words, weight_scales, bias, 
                 for m in range(2):
                     transpose_and_regroup(s + 1, m)
             if 0 <= s < STEPS:
-                for m in range(2):
-                    multiply(s, m)
+                multiply(s)
                 copy_sums(s)
             if s >= 1:
                 differences(s - 1)

@@ -35,6 +35,10 @@ def place(step):
     return rt, 2 * u_high + u_low
 
 
+def all_from_psum(step):
+    return step >= STEPS_OF_A_HALF
+
+
 def tile_iwht3layer_pa_t_e_kernel(tc, trans, weight_words, weight_scales, bias, out):
     nc = tc.nc
 
@@ -47,7 +51,7 @@ def tile_iwht3layer_pa_t_e_kernel(tc, trans, weight_words, weight_scales, bias, 
         w_pool = ctx.enter_context(tc.tile_pool(name="w", bufs=SIDE))
         x_pool = ctx.enter_context(tc.tile_pool(name="x", bufs=(STEPS_LOADED_AHEAD + 1) * SIDE))
         quant_pool = ctx.enter_context(tc.tile_pool(name="quant", bufs=3))
-        stage_pool = ctx.enter_context(tc.tile_pool(name="stage", bufs=5))
+        stage_pool = ctx.enter_context(tc.tile_pool(name="stage", bufs=4))
         stage3_pool = ctx.enter_context(tc.tile_pool(name="stage3", bufs=ROW_TILES + 2))
         pixel_pool = ctx.enter_context(tc.tile_pool(name="pixel", bufs=6))
         flip_psum = ctx.enter_context(tc.psum_pool(name="flip", bufs=SIDE))
@@ -144,29 +148,47 @@ def tile_iwht3layer_pa_t_e_kernel(tc, trans, weight_words, weight_scales, bias, 
                     stop=stop,
                 )
 
-            for acc, members in (
-                (bank_b[:, 0:C_OUT], (2, 3)),
-                (bank_b[:, C_OUT : 2 * C_OUT], (1, 2)),
-                (bank_a[:, 0:C_OUT], (1, 3)),
-                (bank_a[:, C_OUT : 2 * C_OUT], (0, 1, 2, 3)),
-            ):
+            left, right = slice(0, C_OUT), slice(C_OUT, 2 * C_OUT)
+            if all_from_psum(step):
+                groups = ((bank_b[:, left], (2, 3)), (bank_b[:, right], (1, 2)), (bank_a[:, left], (1, 3)), (bank_a[:, right], (0, 1, 2, 3)))
+            else:
+                groups = ((bank_a[:, left], (0, 1)), (bank_b[:, left], (1,)), (bank_a[:, right], (2, 3)), (bank_b[:, right], (3,)))
+            for acc, members in groups:
                 for v in members:
                     for g in range(PASSES):
                         mx_pass(acc, v, g, start=(v == members[0] and g == 0), stop=(v == members[-1] and g == PASSES - 1))
 
         def copy_sums(step):
-            stage2 = stage_pool.tile([P, SIDE, C_OUT], F32)
-            stage2_tiles[step] = stage2
-            if place(step)[1] != 0:
+            if all_from_psum(step):
+                stage2 = stage_pool.tile([P, SIDE, C_OUT], F32)
+                stage2_tiles[step] = stage2
                 nc.scalar.activation(out=stage2[:, 0, :], in_=y_banks[step][0][:, C_OUT : 2 * C_OUT], func=COPY, scale=1.0 / 16.0)
+                return
+            stage1 = stage_pool.tile([P, SIDE, C_OUT], F32)
+            nc.scalar.activation(
+                out=stage1[:, 0:SIDE:2, :],
+                in_=y_banks[step][0][:].rearrange("p (m k) -> p m k", m=2),
+                func=COPY,
+                scale=1.0 / 16.0,
+            )
+            stage1_tiles[step] = stage1
 
         def differences(step):
-            stage2 = stage2_tiles[step]
             bank_a, bank_b = y_banks[step]
-            if place(step)[1] == 0:
+            if not all_from_psum(step):
+                stage1 = stage1_tiles[step]
+                if place(step)[1] == 0:
+                    nc.vector.tensor_tensor(out=stage1[:, 0, :], in0=stage1[:, 0, :], in1=bias_sb[:], op=ADD)
                 nc.vector.scalar_tensor_tensor(
-                    out=stage2[:, 0, :], in0=bank_a[:, C_OUT : 2 * C_OUT], scalar=1.0 / 16.0, in1=bias_sb[:], op0=MULT, op1=ADD
+                    out=stage1[:, 1:SIDE:2, :],
+                    in0=bank_b[:].rearrange("p (m k) -> p m k", m=2),
+                    scalar=-2.0 / 16.0,
+                    in1=stage1[:, 0:SIDE:2, :],
+                    op0=MULT,
+                    op1=ADD,
                 )
+                return
+            stage2 = stage2_tiles[step]
             nc.vector.scalar_tensor_tensor(
                 out=stage2[:, 1, :], in0=bank_a[:, 0:C_OUT], scalar=-2.0 / 16.0, in1=stage2[:, 0, :], op0=MULT, op1=ADD
             )
@@ -185,6 +207,11 @@ def tile_iwht3layer_pa_t_e_kernel(tc, trans, weight_words, weight_scales, bias, 
 
         def later_butterflies(step):
             rt, u = place(step)
+            if not all_from_psum(step):
+                stage1 = stage1_tiles[step]
+                stage2 = stage_pool.tile([P, SIDE, C_OUT], F32)
+                butterfly(stage2[:, 0:2, :], stage2[:, 2:4, :], stage1[:, 0:2, :], stage1[:, 2:4, :])
+                stage2_tiles[step] = stage2
             stage2 = stage2_tiles[step]
             if u % 2 == 0:
                 return

@@ -60,8 +60,12 @@ def tile_iwht3layer_pa_t_e_kernel(tc, trans, weight_words, weight_scales, bias, 
         ident = const.tile([P, P], F32)
         make_identity(nc, ident[:])
 
-        bias_sb = const.tile([P, C_OUT], BF16)
-        nc.scalar.dma_start(out=bias_sb[:], in_=bias.rearrange("a b c k -> (a b c k)").partition_broadcast(P))
+        ones = const.tile([P, P], BF16)
+        nc.gpsimd.memset(ones[:], 1.0)
+        bias_row = const.tile([P, C_OUT], BF16)
+        nc.gpsimd.memset(bias_row[:], 0.0)
+        nc.scalar.dma_start(out=bias_row[0:1, :], in_=bias.rearrange("a b c k -> (a b c) k"))
+        bias_sb = const.tile([P, C_OUT], F32)
 
         w_planes = const.tile([P, SIDE * SIDE * PASSES, C_OUT], U8, align_bytes=64)
         nc.vector.memset(w_planes[:].bitcast(I32), 0)
@@ -77,11 +81,12 @@ def tile_iwht3layer_pa_t_e_kernel(tc, trans, weight_words, weight_scales, bias, 
         stage2_tiles = {}
         stage3_tiles = {}
 
-        def load_weight_scales():
+        def load_weight_scales(half):
+            passes = slice(half * 2 * SIDE * PASSES, (half + 1) * 2 * SIDE * PASSES)
             for r in range(4):
                 nc.sync.dma_start(
-                    out=w_planes[r : P : 32, :, :].bitcast(I32),
-                    in_=weight_scales[:, r : 16 : 4, :].rearrange("g q n -> q g n").bitcast(I32),
+                    out=w_planes[r : P : 32, passes, :].bitcast(I32),
+                    in_=weight_scales[passes, r : 16 : 4, :].rearrange("g q n -> q g n").bitcast(I32),
                 )
 
         def load_weight_words(u):
@@ -90,17 +95,29 @@ def tile_iwht3layer_pa_t_e_kernel(tc, trans, weight_words, weight_scales, bias, 
             nc.sync.dma_start(out=w_words[:].bitcast(I32), in_=w_dram[:, first : first + SIDE * PASSES, :].bitcast(I32))
             w_tiles[u] = w_words
 
-        def load_step(step):
+        def load_rows(step):
             rt, u = place(step)
             x_tiles[step] = []
             for v in range(SIDE):
                 x_raw = x_pool.tile([P, C_IN], BF16)
                 nc.sync.dma_start(out=x_raw[:], in_=x_dram[u, v, rt])
                 x_tiles[step].append(x_raw)
+
+        def load_step(step):
             if step == 0:
-                load_weight_scales()
+                load_rows(0)
+            if step + 1 < STEPS:
+                load_rows(step + 1)
+            rt, u = place(step)
             if rt == 0:
+                if u % 2 == 0:
+                    load_weight_scales(u // 2)
                 load_weight_words(u)
+
+        def spread_bias():
+            flipped = flip_psum.tile([P, C_IN // 2], F32)
+            nc.tensor.matmul(flipped[:, 0:C_OUT], lhsT=ones[:], rhs=bias_row[:], start=True, stop=True)
+            nc.scalar.copy(out=bias_sb[:], in_=flipped[:, 0:C_OUT])
 
         def transpose_and_regroup(step, m):
             if m == 0:
@@ -239,15 +256,17 @@ def tile_iwht3layer_pa_t_e_kernel(tc, trans, weight_words, weight_scales, bias, 
                 )
                 nc.sync.dma_start(out=out_dram[p, rt], in_=pixels[:])
 
-        for step in range(STEPS_LOADED_AHEAD):
+        for step in range(STEPS_LOADED_AHEAD - 1):
             load_step(step)
 
         for s in range(-1, STEPS + 1):
-            if s + STEPS_LOADED_AHEAD + 1 < STEPS:
-                load_step(s + STEPS_LOADED_AHEAD + 1)
+            if s + STEPS_LOADED_AHEAD < STEPS:
+                load_step(s + STEPS_LOADED_AHEAD)
             if s + 1 < STEPS:
                 for m in range(2):
                     transpose_and_regroup(s + 1, m)
+            if s == -1:
+                spread_bias()
             if 0 <= s < STEPS:
                 multiply(s)
                 copy_sums(s)

@@ -24,19 +24,24 @@ ROW_TILES = 4
 STEPS = ROW_TILES * SIDE
 STEPS_OF_A_HALF = STEPS // 2
 STEPS_LOADED_AHEAD = 3
+PAIR_STEPS = 4
+WAITING_A_TURN = 3
 ROW_COLS = SIDE * C_OUT
 
 FLOPS = 2 * SIDE * SIDE * ROW_TILES * P * C_IN * C_OUT
 
 
 def place(step):
-    u_high, rest = divmod(step, STEPS_OF_A_HALF)
-    rt, u_low = divmod(rest, 2)
+    pair, u_low = divmod(step, 2)
+    if pair < 4:
+        u_high, rt = divmod(pair, 2)
+    else:
+        rt, u_high = divmod(pair, 2)
     return rt, 2 * u_high + u_low
 
 
 def all_from_psum(step):
-    return step >= STEPS_OF_A_HALF
+    return step >= PAIR_STEPS
 
 
 def tile_iwht3layer_pa_t_e_kernel(tc, trans, weight_words, weight_scales, bias, out):
@@ -51,8 +56,8 @@ def tile_iwht3layer_pa_t_e_kernel(tc, trans, weight_words, weight_scales, bias, 
         w_pool = ctx.enter_context(tc.tile_pool(name="w", bufs=SIDE))
         x_pool = ctx.enter_context(tc.tile_pool(name="x", bufs=(STEPS_LOADED_AHEAD + 1) * SIDE))
         quant_pool = ctx.enter_context(tc.tile_pool(name="quant", bufs=3))
-        stage_pool = ctx.enter_context(tc.tile_pool(name="stage", bufs=4))
-        stage3_pool = ctx.enter_context(tc.tile_pool(name="stage3", bufs=ROW_TILES + 2))
+        stage_pool = ctx.enter_context(tc.tile_pool(name="stage", bufs=6))
+        stage3_pool = ctx.enter_context(tc.tile_pool(name="stage3", bufs=8))
         pixel_pool = ctx.enter_context(tc.tile_pool(name="pixel", bufs=6))
         flip_psum = ctx.enter_context(tc.psum_pool(name="flip", bufs=SIDE))
         y_psum = ctx.enter_context(tc.psum_pool(name="y", bufs=2))
@@ -67,8 +72,11 @@ def tile_iwht3layer_pa_t_e_kernel(tc, trans, weight_words, weight_scales, bias, 
         nc.scalar.dma_start(out=bias_row[0:1, :], in_=bias.rearrange("a b c k -> (a b c) k"))
         bias_sb = const.tile([P, C_OUT], F32)
 
-        w_planes = const.tile([P, SIDE * SIDE * PASSES, C_OUT], U8, align_bytes=64)
-        nc.vector.memset(w_planes[:].bitcast(I32), 0)
+        planes_low = const.tile([P, 2 * SIDE * PASSES, C_OUT], U8, align_bytes=64)
+        nc.vector.memset(planes_low[:].bitcast(I32), 0)
+        planes_high = const.tile([P, 2 * SIDE * PASSES, C_OUT], U8, align_bytes=64)
+        nc.vector.memset(planes_high[:].bitcast(I32), 0)
+        w_planes = (planes_low, planes_high)
 
         ctx.enter_context(tc.manual_schedule())
 
@@ -85,7 +93,7 @@ def tile_iwht3layer_pa_t_e_kernel(tc, trans, weight_words, weight_scales, bias, 
             passes = slice(half * 2 * SIDE * PASSES, (half + 1) * 2 * SIDE * PASSES)
             for r in range(4):
                 nc.sync.dma_start(
-                    out=w_planes[r : P : 32, passes, :].bitcast(I32),
+                    out=w_planes[half][r : P : 32, :, :].bitcast(I32),
                     in_=weight_scales[passes, r : 16 : 4, :].rearrange("g q n -> q g n").bitcast(I32),
                 )
 
@@ -160,7 +168,7 @@ def tile_iwht3layer_pa_t_e_kernel(tc, trans, weight_words, weight_scales, bias, 
                     lhsT=codes[:, rows].bitcast(FP8X4),
                     lhsT_scale=x_scales[:, rows],
                     rhs=w_tiles[u][:, v * PASSES + g, :].bitcast(FP8X4),
-                    rhs_scale=w_planes[:, (u * SIDE + v) * PASSES + g, :],
+                    rhs_scale=w_planes[u // 2][:, ((u % 2) * SIDE + v) * PASSES + g, :],
                     start=start,
                     stop=stop,
                 )
@@ -179,7 +187,8 @@ def tile_iwht3layer_pa_t_e_kernel(tc, trans, weight_words, weight_scales, bias, 
             if all_from_psum(step):
                 stage2 = stage_pool.tile([P, SIDE, C_OUT], F32)
                 stage2_tiles[step] = stage2
-                nc.scalar.activation(out=stage2[:, 0, :], in_=y_banks[step][0][:, C_OUT : 2 * C_OUT], func=COPY, scale=1.0 / 16.0)
+                if place(step)[1] != 0:
+                    nc.scalar.activation(out=stage2[:, 0, :], in_=y_banks[step][0][:, C_OUT : 2 * C_OUT], func=COPY, scale=1.0 / 16.0)
                 return
             stage1 = stage_pool.tile([P, SIDE, C_OUT], F32)
             nc.scalar.activation(
@@ -190,12 +199,26 @@ def tile_iwht3layer_pa_t_e_kernel(tc, trans, weight_words, weight_scales, bias, 
             )
             stage1_tiles[step] = stage1
 
+        def add_bias(step):
+            if place(step)[1] != 0:
+                return
+            if all_from_psum(step):
+                nc.vector.scalar_tensor_tensor(
+                    out=stage2_tiles[step][:, 0, :],
+                    in0=y_banks[step][0][:, C_OUT : 2 * C_OUT],
+                    scalar=1.0 / 16.0,
+                    in1=bias_sb[:],
+                    op0=MULT,
+                    op1=ADD,
+                )
+            else:
+                stage1 = stage1_tiles[step]
+                nc.vector.tensor_tensor(out=stage1[:, 0, :], in0=stage1[:, 0, :], in1=bias_sb[:], op=ADD)
+
         def differences(step):
             bank_a, bank_b = y_banks[step]
             if not all_from_psum(step):
                 stage1 = stage1_tiles[step]
-                if place(step)[1] == 0:
-                    nc.vector.tensor_tensor(out=stage1[:, 0, :], in0=stage1[:, 0, :], in1=bias_sb[:], op=ADD)
                 nc.vector.scalar_tensor_tensor(
                     out=stage1[:, 1:SIDE:2, :],
                     in0=bank_b[:].rearrange("p (m k) -> p m k", m=2),
@@ -218,43 +241,53 @@ def tile_iwht3layer_pa_t_e_kernel(tc, trans, weight_words, weight_scales, bias, 
                 op1=ADD,
             )
 
-        def butterfly(plus, minus, first, second):
-            nc.vector.tensor_tensor(out=plus, in0=first, in1=second, op=ADD)
-            nc.vector.tensor_tensor(out=minus, in0=first, in1=second, op=SUBTRACT)
+        def second_butterfly(step):
+            stage1 = stage1_tiles[step]
+            stage2 = stage_pool.tile([P, SIDE, C_OUT], F32)
+            nc.vector.tensor_tensor(out=stage2[:, 0:2, :], in0=stage1[:, 0:2, :], in1=stage1[:, 2:4, :], op=ADD)
+            nc.vector.tensor_tensor(out=stage2[:, 2:4, :], in0=stage1[:, 0:2, :], in1=stage1[:, 2:4, :], op=SUBTRACT)
+            stage2_tiles[step] = stage2
 
-        def later_butterflies(step):
+        def third_butterfly(step, low_p):
+            rt, u = place(step)
+            stage3 = stage3_pool.tile([P, ROW_COLS], F32)
+            nc.vector.tensor_tensor(
+                out=stage3[:],
+                in0=stage2_tiles[step - 1][:].rearrange("p q k -> p (q k)"),
+                in1=stage2_tiles[step][:].rearrange("p q k -> p (q k)"),
+                op=(ADD if low_p == 0 else SUBTRACT),
+            )
+            stage3_tiles[(rt, low_p, u // 2)] = stage3
+
+        def last_butterfly(rt, p):
+            pixels = pixel_pool.tile([P, ROW_COLS], F32)
+            nc.vector.tensor_tensor(
+                out=pixels[:],
+                in0=stage3_tiles[(rt, p % 2, 0)][:],
+                in1=stage3_tiles[(rt, p % 2, 1)][:],
+                op=(ADD if p < 2 else SUBTRACT),
+            )
+            nc.sync.dma_start(out=out_dram[p, rt], in_=pixels[:])
+
+        waiting = []
+
+        def enqueue(step):
             rt, u = place(step)
             if not all_from_psum(step):
-                stage1 = stage1_tiles[step]
-                stage2 = stage_pool.tile([P, SIDE, C_OUT], F32)
-                butterfly(stage2[:, 0:2, :], stage2[:, 2:4, :], stage1[:, 0:2, :], stage1[:, 2:4, :])
-                stage2_tiles[step] = stage2
-            stage2 = stage2_tiles[step]
-            if u % 2 == 0:
-                return
+                waiting.append(lambda: second_butterfly(step))
+            if u % 2 == 1:
+                waiting.append(lambda: third_butterfly(step, 0))
+                waiting.append(lambda: third_butterfly(step, 1))
+            if u == SIDE - 1:
+                for p in (0, 2, 1, 3):
+                    waiting.append(lambda p=p: last_butterfly(rt, p))
 
-            stage3_plus = stage3_pool.tile([P, ROW_COLS], F32)
-            stage3_minus = stage3_pool.tile([P, ROW_COLS], F32)
-            butterfly(
-                stage3_plus[:],
-                stage3_minus[:],
-                stage2_tiles[step - 1][:].rearrange("p q k -> p (q k)"),
-                stage2[:].rearrange("p q k -> p (q k)"),
-            )
-            stage3_tiles[(rt, 0, u // 2)] = stage3_plus
-            stage3_tiles[(rt, 1, u // 2)] = stage3_minus
-            if u < SIDE - 1:
-                return
-
-            for p in range(SIDE):
-                pixels = pixel_pool.tile([P, ROW_COLS], F32)
-                nc.vector.tensor_tensor(
-                    out=pixels[:],
-                    in0=stage3_tiles[(rt, p % 2, 0)][:],
-                    in1=stage3_tiles[(rt, p % 2, 1)][:],
-                    op=(ADD if p < 2 else SUBTRACT),
-                )
-                nc.sync.dma_start(out=out_dram[p, rt], in_=pixels[:])
+        def make_waiting(limit):
+            for operation in waiting[:limit]:
+                operation()
+            rest = waiting[limit:]
+            waiting.clear()
+            waiting.extend(rest)
 
         for step in range(STEPS_LOADED_AHEAD - 1):
             load_step(step)
@@ -271,8 +304,10 @@ def tile_iwht3layer_pa_t_e_kernel(tc, trans, weight_words, weight_scales, bias, 
                 multiply(s)
                 copy_sums(s)
             if s >= 1:
+                add_bias(s - 1)
+                make_waiting(1)
                 differences(s - 1)
+                enqueue(s - 1)
             if s + 1 < STEPS:
                 quantise(s + 1)
-            if s >= 1:
-                later_butterflies(s - 1)
+            make_waiting(WAITING_A_TURN - 1 if s < STEPS else len(waiting))

@@ -65,8 +65,10 @@ def tile_iwht3layer_pa_t_e_kernel(tc, trans, weight_words, weight_scales, bias, 
         ident = const.tile([P, P], F32)
         make_identity(nc, ident[:])
 
-        ones = const.tile([P, P], BF16)
+        ones = const.tile([P, 4 * P], BF16)
         nc.gpsimd.memset(ones[:], 1.0)
+        table_warmer = const.tile([P, 1], F32)
+        nc.scalar.activation(out=table_warmer[:], in_=ones[:, 0:1], func=COPY, scale=1.0 / 16.0)
         bias_row = const.tile([P, C_OUT], BF16)
         nc.gpsimd.memset(bias_row[:], 0.0)
         nc.scalar.dma_start(out=bias_row[0:1, :], in_=bias.rearrange("a b c k -> (a b c) k"))
@@ -122,9 +124,14 @@ def tile_iwht3layer_pa_t_e_kernel(tc, trans, weight_words, weight_scales, bias, 
                     load_weight_scales(u // 2)
                 load_weight_words(u)
 
+        def warm_up(count):
+            flipped = flip_psum.tile([P, C_IN // 2], F32)
+            for i in range(count):
+                nc.tensor.matmul(flipped[:], lhsT=ones[:, 0:P], rhs=ones[:], start=True, stop=True)
+
         def spread_bias():
             flipped = flip_psum.tile([P, C_IN // 2], F32)
-            nc.tensor.matmul(flipped[:, 0:C_OUT], lhsT=ones[:], rhs=bias_row[:], start=True, stop=True)
+            nc.tensor.matmul(flipped[:, 0:C_OUT], lhsT=ones[:, 0:P], rhs=bias_row[:], start=True, stop=True)
             nc.scalar.copy(out=bias_sb[:], in_=flipped[:, 0:C_OUT])
 
         def transpose_and_regroup(step, m):
@@ -292,6 +299,7 @@ def tile_iwht3layer_pa_t_e_kernel(tc, trans, weight_words, weight_scales, bias, 
         for step in range(STEPS_LOADED_AHEAD - 1):
             load_step(step)
 
+        warm_up(4)
         for s in range(-1, STEPS + 1):
             if s + STEPS_LOADED_AHEAD < STEPS:
                 load_step(s + STEPS_LOADED_AHEAD)
@@ -300,6 +308,7 @@ def tile_iwht3layer_pa_t_e_kernel(tc, trans, weight_words, weight_scales, bias, 
                     transpose_and_regroup(s + 1, m)
             if s == -1:
                 spread_bias()
+                warm_up(2)
             if 0 <= s < STEPS:
                 multiply(s)
                 copy_sums(s)

@@ -24,7 +24,7 @@ ROW_TILES = 4
 STEPS = ROW_TILES * SIDE
 STEPS_OF_A_HALF = STEPS // 2
 STEPS_LOADED_AHEAD = 3
-PAIR_STEPS = 4
+PAIR_STEPS = 8
 WAITING_A_TURN = 3
 ROW_COLS = SIDE * C_OUT
 

@@ -24,7 +24,8 @@ ROW_TILES = 4
 STEPS = ROW_TILES * SIDE
 STEPS_OF_A_HALF = STEPS // 2
 STEPS_LOADED_AHEAD = 3
-PAIR_STEPS = 8
+PAIR_STEPS = 4
+SORTED = (0, 2)
 WAITING_A_TURN = 3
 ROW_COLS = SIDE * C_OUT
 
@@ -55,6 +56,7 @@ def tile_iwht3layer_pa_t_e_kernel(tc, trans, weight_words, weight_scales, bias, 
         const = ctx.enter_context(tc.tile_pool(name="const", bufs=1))
         w_pool = ctx.enter_context(tc.tile_pool(name="w", bufs=SIDE))
         x_pool = ctx.enter_context(tc.tile_pool(name="x", bufs=(STEPS_LOADED_AHEAD + 1) * SIDE))
+        sorted_pool = ctx.enter_context(tc.tile_pool(name="sorted", bufs=2 * len(SORTED)))
         quant_pool = ctx.enter_context(tc.tile_pool(name="quant", bufs=3))
         stage_pool = ctx.enter_context(tc.tile_pool(name="stage", bufs=6))
         stage3_pool = ctx.enter_context(tc.tile_pool(name="stage3", bufs=8))
@@ -83,6 +85,7 @@ def tile_iwht3layer_pa_t_e_kernel(tc, trans, weight_words, weight_scales, bias, 
         ctx.enter_context(tc.manual_schedule())
 
         x_tiles = {}
+        sorted_tiles = {}
         w_tiles = {}
         grouped_tiles = {}
         code_tiles = {}
@@ -134,18 +137,31 @@ def tile_iwht3layer_pa_t_e_kernel(tc, trans, weight_words, weight_scales, bias, 
             nc.tensor.matmul(flipped[:, 0:C_OUT], lhsT=ones[:, 0:P], rhs=bias_row[:], start=True, stop=True)
             nc.scalar.copy(out=bias_sb[:], in_=flipped[:, 0:C_OUT])
 
+        def sort_words(step, v):
+            x_sorted = sorted_pool.tile([P, C_IN], BF16)
+            nc.scalar.copy(
+                out=x_sorted[:].bitcast(F32).rearrange("p (g w j) -> p g w j", g=PASSES, w=2),
+                in_=x_tiles[step][v][:].bitcast(F32).rearrange("p (g j w) -> p g w j", g=PASSES, w=2),
+            )
+            sorted_tiles[(step, v)] = x_sorted
+
         def transpose_and_regroup(step, m):
             if m == 0:
                 grouped = quant_pool.tile([P, SIDE * C_IN], BF16, align_bytes=64)
                 grouped_tiles[step] = grouped
             for v in (2 * m, 2 * m + 1):
-                x_words = x_tiles[step][v][:].bitcast(F32)
+                is_sorted = (step, v) in sorted_tiles
+                x_words = (sorted_tiles[(step, v)] if is_sorted else x_tiles[step][v])[:].bitcast(F32)
                 flipped = flip_psum.tile([P, C_IN // 2], F32)
                 for g in range(PASSES):
                     for w in range(2):
                         nc.tensor.transpose(
                             flipped[:, (2 * g + w) * P : (2 * g + w + 1) * P],
-                            x_words[:, (K_PASS // 2) * g + w : (K_PASS // 2) * (g + 1) : 2],
+                            (
+                                x_words[:, (2 * g + w) * P : (2 * g + w + 1) * P]
+                                if is_sorted
+                                else x_words[:, (K_PASS // 2) * g + w : (K_PASS // 2) * (g + 1) : 2]
+                            ),
                             ident[:],
                         )
                 nc.scalar.copy(
@@ -309,6 +325,9 @@ def tile_iwht3layer_pa_t_e_kernel(tc, trans, weight_words, weight_scales, bias, 
             if s == -1:
                 spread_bias()
                 warm_up(2)
+            if s + 2 < STEPS:
+                for v in SORTED:
+                    sort_words(s + 2, v)
             if 0 <= s < STEPS:
                 multiply(s)
                 copy_sums(s)

@@ -24,7 +24,7 @@ ROW_TILES = 4
 STEPS = ROW_TILES * SIDE
 STEPS_OF_A_HALF = STEPS // 2
 STEPS_LOADED_AHEAD = 3
-PAIR_STEPS = 4
+PAIR_STEPS = 6
 SORTED = (0, 2)
 WAITING_A_TURN = 3
 ROW_COLS = SIDE * C_OUT

@@ -24,9 +24,29 @@ ROW_TILES = 4
 STEPS = ROW_TILES * SIDE
 STEPS_OF_A_HALF = STEPS // 2
 STEPS_LOADED_AHEAD = 3
-PAIR_STEPS = 6
-SORTED = (0, 2)
-WAITING_A_TURN = 3
+LAG = 2
+TAIL = 1
+PAIRS = (0, 1, 2, 3, 4, 5)
+
+
+def sorted_of(step):
+    if step == 0:
+        return ()
+    return (0, 2) if step in PAIRS else (0, 1, 2)
+
+
+def waits(s):
+    return (1, 1, 1) if s < 7 else (1, 0, 2)
+
+
+def vevac(step):
+    return ()
+
+
+def shared_at(s):
+    return True
+
+
 ROW_COLS = SIDE * C_OUT
 
 FLOPS = 2 * SIDE * SIDE * ROW_TILES * P * C_IN * C_OUT
@@ -42,7 +62,7 @@ def place(step):
 
 
 def all_from_psum(step):
-    return step >= PAIR_STEPS
+    return step not in PAIRS
 
 
 def tile_iwht3layer_pa_t_e_kernel(tc, trans, weight_words, weight_scales, bias, out):
@@ -56,7 +76,7 @@ def tile_iwht3layer_pa_t_e_kernel(tc, trans, weight_words, weight_scales, bias, 
         const = ctx.enter_context(tc.tile_pool(name="const", bufs=1))
         w_pool = ctx.enter_context(tc.tile_pool(name="w", bufs=SIDE))
         x_pool = ctx.enter_context(tc.tile_pool(name="x", bufs=(STEPS_LOADED_AHEAD + 1) * SIDE))
-        sorted_pool = ctx.enter_context(tc.tile_pool(name="sorted", bufs=2 * len(SORTED)))
+        sorted_pool = ctx.enter_context(tc.tile_pool(name="sorted", bufs=8))
         quant_pool = ctx.enter_context(tc.tile_pool(name="quant", bufs=3))
         stage_pool = ctx.enter_context(tc.tile_pool(name="stage", bufs=6))
         stage3_pool = ctx.enter_context(tc.tile_pool(name="stage3", bufs=8))
@@ -73,7 +93,6 @@ def tile_iwht3layer_pa_t_e_kernel(tc, trans, weight_words, weight_scales, bias, 
         nc.scalar.activation(out=table_warmer[:], in_=ones[:, 0:1], func=COPY, scale=1.0 / 16.0)
         bias_row = const.tile([P, C_OUT], BF16)
         nc.gpsimd.memset(bias_row[:], 0.0)
-        nc.scalar.dma_start(out=bias_row[0:1, :], in_=bias.rearrange("a b c k -> (a b c) k"))
         bias_sb = const.tile([P, C_OUT], F32)
 
         planes_low = const.tile([P, 2 * SIDE * PASSES, C_OUT], U8, align_bytes=64)
@@ -119,6 +138,7 @@ def tile_iwht3layer_pa_t_e_kernel(tc, trans, weight_words, weight_scales, bias, 
         def load_step(step):
             if step == 0:
                 load_rows(0)
+                nc.sync.dma_start(out=bias_row[0:1, :], in_=bias.rearrange("a b c k -> (a b c) k"))
             if step + 1 < STEPS:
                 load_rows(step + 1)
             rt, u = place(step)
@@ -164,7 +184,7 @@ def tile_iwht3layer_pa_t_e_kernel(tc, trans, weight_words, weight_scales, bias, 
                             ),
                             ident[:],
                         )
-                nc.scalar.copy(
+                (nc.vector.tensor_copy if v in vevac(step) else nc.scalar.copy)(
                     out=grouped_tiles[step][:, v * C_IN : (v + 1) * C_IN]
                     .bitcast(F32)
                     .rearrange("p (g r w) -> p g r w", g=PASSES, w=2),
@@ -177,12 +197,14 @@ def tile_iwht3layer_pa_t_e_kernel(tc, trans, weight_words, weight_scales, bias, 
             nc.vector.quantize_mx(out=codes[:].bitcast(FP8X4), scales=x_scales[:], in_=grouped_tiles[step][:])
             code_tiles[step] = (codes, x_scales)
 
-        def multiply(step):
+        def multiply(step, halves=(0, 1)):
             u = place(step)[1]
             codes, x_scales = code_tiles[step]
-            bank_a = y_psum.tile([P, 2 * C_OUT], F32)
-            bank_b = y_psum.tile([P, 2 * C_OUT], F32)
-            y_banks[step] = (bank_a, bank_b)
+            if 0 in halves:
+                bank_a = y_psum.tile([P, 2 * C_OUT], F32)
+                bank_b = y_psum.tile([P, 2 * C_OUT], F32)
+                y_banks[step] = (bank_a, bank_b)
+            bank_a, bank_b = y_banks[step]
 
             def mx_pass(acc, v, g, start, stop):
                 rows = slice((v * PASSES + g) * P, (v * PASSES + g + 1) * P)
@@ -198,10 +220,10 @@ def tile_iwht3layer_pa_t_e_kernel(tc, trans, weight_words, weight_scales, bias, 
 
             left, right = slice(0, C_OUT), slice(C_OUT, 2 * C_OUT)
             if all_from_psum(step):
-                groups = ((bank_b[:, left], (2, 3)), (bank_b[:, right], (1, 2)), (bank_a[:, left], (1, 3)), (bank_a[:, right], (0, 1, 2, 3)))
+                groups = ((bank_a[:, left], (1, 3)), (bank_a[:, right], (0, 1, 2, 3)), (bank_b[:, left], (2, 3)), (bank_b[:, right], (1, 2)))
             else:
-                groups = ((bank_a[:, left], (0, 1)), (bank_b[:, left], (1,)), (bank_a[:, right], (2, 3)), (bank_b[:, right], (3,)))
-            for acc, members in groups:
+                groups = ((bank_a[:, left], (0, 1)), (bank_a[:, right], (2, 3)), (bank_b[:, left], (1,)), (bank_b[:, right], (3,)))
+            for acc, members in groups[2 * halves[0] : 2 * halves[-1] + 2]:
                 for v in members:
                     for g in range(PASSES):
                         mx_pass(acc, v, g, start=(v == members[0] and g == 0), stop=(v == members[-1] and g == PASSES - 1))
@@ -238,7 +260,7 @@ def tile_iwht3layer_pa_t_e_kernel(tc, trans, weight_words, weight_scales, bias, 
                 stage1 = stage1_tiles[step]
                 nc.vector.tensor_tensor(out=stage1[:, 0, :], in0=stage1[:, 0, :], in1=bias_sb[:], op=ADD)
 
-        def differences(step):
+        def differences(step, parts=(0, 1)):
             bank_a, bank_b = y_banks[step]
             if not all_from_psum(step):
                 stage1 = stage1_tiles[step]
@@ -252,17 +274,19 @@ def tile_iwht3layer_pa_t_e_kernel(tc, trans, weight_words, weight_scales, bias, 
                 )
                 return
             stage2 = stage2_tiles[step]
-            nc.vector.scalar_tensor_tensor(
-                out=stage2[:, 1, :], in0=bank_a[:, 0:C_OUT], scalar=-2.0 / 16.0, in1=stage2[:, 0, :], op0=MULT, op1=ADD
-            )
-            nc.vector.scalar_tensor_tensor(
-                out=stage2[:, 2:4, :],
-                in0=bank_b[:].rearrange("p (m k) -> p m k", m=2),
-                scalar=-2.0 / 16.0,
-                in1=stage2[:, 0:1, :].to_broadcast([P, 2, C_OUT]),
-                op0=MULT,
-                op1=ADD,
-            )
+            if 0 in parts:
+                nc.vector.scalar_tensor_tensor(
+                    out=stage2[:, 1, :], in0=bank_a[:, 0:C_OUT], scalar=-2.0 / 16.0, in1=stage2[:, 0, :], op0=MULT, op1=ADD
+                )
+            if 1 in parts:
+                nc.vector.scalar_tensor_tensor(
+                    out=stage2[:, 2:4, :],
+                    in0=bank_b[:].rearrange("p (m k) -> p m k", m=2),
+                    scalar=-2.0 / 16.0,
+                    in1=stage2[:, 0:1, :].to_broadcast([P, 2, C_OUT]),
+                    op0=MULT,
+                    op1=ADD,
+                )
 
         def second_butterfly(step):
             stage1 = stage1_tiles[step]
@@ -271,24 +295,29 @@ def tile_iwht3layer_pa_t_e_kernel(tc, trans, weight_words, weight_scales, bias, 
             nc.vector.tensor_tensor(out=stage2[:, 2:4, :], in0=stage1[:, 0:2, :], in1=stage1[:, 2:4, :], op=SUBTRACT)
             stage2_tiles[step] = stage2
 
-        def third_butterfly(step, low_p):
+        def row_operation(out_row, in0, in1, op, shared):
+            end = 3 * C_OUT + 8 if shared else ROW_COLS
+            nc.vector.tensor_tensor(out=out_row[:, 0:end], in0=in0[:, 0:end], in1=in1[:, 0:end], op=op)
+            if shared:
+                rest = slice(3 * C_OUT, ROW_COLS)
+                nc.gpsimd.tensor_tensor(out=out_row[:, rest], in0=in0[:, rest], in1=in1[:, rest], op=op)
+
+        def third_butterfly(step, low_p, shared):
             rt, u = place(step)
             stage3 = stage3_pool.tile([P, ROW_COLS], F32)
-            nc.vector.tensor_tensor(
-                out=stage3[:],
-                in0=stage2_tiles[step - 1][:].rearrange("p q k -> p (q k)"),
-                in1=stage2_tiles[step][:].rearrange("p q k -> p (q k)"),
-                op=(ADD if low_p == 0 else SUBTRACT),
+            row_operation(
+                stage3,
+                stage2_tiles[step - 1][:].rearrange("p q k -> p (q k)"),
+                stage2_tiles[step][:].rearrange("p q k -> p (q k)"),
+                ADD if low_p == 0 else SUBTRACT,
+                shared,
             )
             stage3_tiles[(rt, low_p, u // 2)] = stage3
 
-        def last_butterfly(rt, p):
+        def last_butterfly(rt, p, shared):
             pixels = pixel_pool.tile([P, ROW_COLS], F32)
-            nc.vector.tensor_tensor(
-                out=pixels[:],
-                in0=stage3_tiles[(rt, p % 2, 0)][:],
-                in1=stage3_tiles[(rt, p % 2, 1)][:],
-                op=(ADD if p < 2 else SUBTRACT),
+            row_operation(
+                pixels, stage3_tiles[(rt, p % 2, 0)], stage3_tiles[(rt, p % 2, 1)], ADD if p < 2 else SUBTRACT, shared
             )
             nc.sync.dma_start(out=out_dram[p, rt], in_=pixels[:])
 
@@ -297,17 +326,17 @@ def tile_iwht3layer_pa_t_e_kernel(tc, trans, weight_words, weight_scales, bias, 
         def enqueue(step):
             rt, u = place(step)
             if not all_from_psum(step):
-                waiting.append(lambda: second_butterfly(step))
+                waiting.append(lambda shared: second_butterfly(step))
             if u % 2 == 1:
-                waiting.append(lambda: third_butterfly(step, 0))
-                waiting.append(lambda: third_butterfly(step, 1))
+                waiting.append(lambda shared: third_butterfly(step, 0, shared))
+                waiting.append(lambda shared: third_butterfly(step, 1, shared))
             if u == SIDE - 1:
                 for p in (0, 2, 1, 3):
-                    waiting.append(lambda p=p: last_butterfly(rt, p))
+                    waiting.append(lambda shared, p=p: last_butterfly(rt, p, shared))
 
-        def make_waiting(limit):
+        def make_waiting(limit, shared=False):
             for operation in waiting[:limit]:
-                operation()
+                operation(shared)
             rest = waiting[limit:]
             waiting.clear()
             waiting.extend(rest)
@@ -316,26 +345,70 @@ def tile_iwht3layer_pa_t_e_kernel(tc, trans, weight_words, weight_scales, bias, 
             load_step(step)
 
         warm_up(4)
-        for s in range(-1, STEPS + 1):
+        for s in range(-1, STEPS if TAIL else STEPS + 1):
+            w0, w1, w2 = waits(s)
             if s + STEPS_LOADED_AHEAD < STEPS:
                 load_step(s + STEPS_LOADED_AHEAD)
+            if LAG == 3 and s >= 1:
+                copy_sums(s - 1)
             if s + 1 < STEPS:
-                for m in range(2):
-                    transpose_and_regroup(s + 1, m)
+                transpose_and_regroup(s + 1, 0)
+            if LAG == 3 and s >= 1:
+                multiply(s - 1, (1,))
+            sorts = sorted_of(s + 2) if s + 2 < STEPS else ()
+            if LAG == 3:
+                for v in sorts[: (len(sorts) + 1) // 2]:
+                    sort_words(s + 2, v)
+            if s + 1 < STEPS:
+                transpose_and_regroup(s + 1, 1)
             if s == -1:
                 spread_bias()
                 warm_up(2)
-            if s + 2 < STEPS:
-                for v in SORTED:
+            if LAG == 3:
+                if 0 <= s < STEPS:
+                    multiply(s, (0,))
+                for v in sorts[(len(sorts) + 1) // 2 :]:
                     sort_words(s + 2, v)
-            if 0 <= s < STEPS:
-                multiply(s)
-                copy_sums(s)
+            else:
+                if 0 <= s < STEPS:
+                    multiply(s)
+                for v in sorts:
+                    sort_words(s + 2, v)
+                if 0 <= s < STEPS:
+                    copy_sums(s)
             if s >= 1:
                 add_bias(s - 1)
-                make_waiting(1)
+                make_waiting(w0, shared=shared_at(s))
                 differences(s - 1)
                 enqueue(s - 1)
+            make_waiting(w1)
             if s + 1 < STEPS:
                 quantise(s + 1)
-            make_waiting(WAITING_A_TURN - 1 if s < STEPS else len(waiting))
+            make_waiting(w2 if s < STEPS - 1 else len(waiting))
+
+        if TAIL:
+            last = STEPS - 1
+            rt = place(last)[0]
+            if LAG == 3:
+                copy_sums(last)
+                multiply(last, (1,))
+            stage3 = [stage3_pool.tile([P, ROW_COLS], F32, name="stage3") for low_p in range(2)]
+            pixels = [pixel_pool.tile([P, ROW_COLS], F32, name="pixels") for p in range(SIDE)]
+            for part in range(2):
+                cols = slice(part * ROW_COLS // 2, (part + 1) * ROW_COLS // 2)
+                differences(last, (part,))
+                for low_p in range(2):
+                    nc.vector.tensor_tensor(
+                        out=stage3[low_p][:, cols],
+                        in0=stage2_tiles[last - 1][:].rearrange("p q k -> p (q k)")[:, cols],
+                        in1=stage2_tiles[last][:].rearrange("p q k -> p (q k)")[:, cols],
+                        op=(ADD if low_p == 0 else SUBTRACT),
+                    )
+                for p in (0, 2, 1, 3):
+                    nc.vector.tensor_tensor(
+                        out=pixels[p][:, cols],
+                        in0=stage3_tiles[(rt, p % 2, 0)][:, cols],
+                        in1=stage3[p % 2][:, cols],
+                        op=(ADD if p < 2 else SUBTRACT),
+                    )
+                    nc.sync.dma_start(out=out_dram[p, rt][:, :, cols], in_=pixels[p][:, cols])

@@ -25,18 +25,32 @@ STEPS = ROW_TILES * SIDE
 STEPS_OF_A_HALF = STEPS // 2
 STEPS_LOADED_AHEAD = 3
 LAG = 2
-TAIL = 1
-PAIRS = (0, 1, 2, 3, 4, 5)
+SPLITD = False
+SKIP = True
+WB = 1
+WARM0 = 4
+WARM1 = 2
+ORDER = ((0, 0), (1, 0), (0, 1), (1, 1), (2, 0), (2, 1), (3, 0), (3, 1))
+R2B = 10
+ACCB = 3
+XB = 4
+EARLY = 0
+HEAD = "x0 b x1 s0 w0 x2 s1 w1 x3"
+LATER = {1: "s2 w2", 2: "s3 w3"}
+SHARE = 256
+TAIL = 4
+
+
+def scheme(step):
+    return "PPPPPQQQQQQQQQQQ"[step]
 
 
 def sorted_of(step):
-    if step == 0:
-        return ()
-    return (0, 2) if step in PAIRS else (0, 1, 2)
+    return () if step < 2 else (0,)
 
 
 def waits(s):
-    return (1, 1, 1) if s < 7 else (1, 0, 2)
+    return (1, 1, 0)
 
 
 def vevac(step):
@@ -44,7 +58,7 @@ def vevac(step):
 
 
 def shared_at(s):
-    return True
+    return False
 
 
 ROW_COLS = SIDE * C_OUT
@@ -54,15 +68,12 @@ FLOPS = 2 * SIDE * SIDE * ROW_TILES * P * C_IN * C_OUT
 
 def place(step):
     pair, u_low = divmod(step, 2)
-    if pair < 4:
-        u_high, rt = divmod(pair, 2)
-    else:
-        rt, u_high = divmod(pair, 2)
+    rt, u_high = ORDER[pair]
     return rt, 2 * u_high + u_low
 
 
 def all_from_psum(step):
-    return step not in PAIRS
+    return scheme(step) != "P"
 
 
 def tile_iwht3layer_pa_t_e_kernel(tc, trans, weight_words, weight_scales, bias, out):
@@ -75,11 +86,12 @@ def tile_iwht3layer_pa_t_e_kernel(tc, trans, weight_words, weight_scales, bias, 
     with ExitStack() as ctx:
         const = ctx.enter_context(tc.tile_pool(name="const", bufs=1))
         w_pool = ctx.enter_context(tc.tile_pool(name="w", bufs=SIDE))
-        x_pool = ctx.enter_context(tc.tile_pool(name="x", bufs=(STEPS_LOADED_AHEAD + 1) * SIDE))
-        sorted_pool = ctx.enter_context(tc.tile_pool(name="sorted", bufs=8))
+        x_pool = ctx.enter_context(tc.tile_pool(name="x", bufs=XB * SIDE))
+        sorted_pool = ctx.enter_context(tc.tile_pool(name="sorted", bufs=4))
         quant_pool = ctx.enter_context(tc.tile_pool(name="quant", bufs=3))
-        stage_pool = ctx.enter_context(tc.tile_pool(name="stage", bufs=6))
-        stage3_pool = ctx.enter_context(tc.tile_pool(name="stage3", bufs=8))
+        stage_pool = ctx.enter_context(tc.tile_pool(name="stage", bufs=4))
+        row_pool = ctx.enter_context(tc.tile_pool(name="row", bufs=R2B))
+        acc_pool = ctx.enter_context(tc.tile_pool(name="acc", bufs=ACCB))
         pixel_pool = ctx.enter_context(tc.tile_pool(name="pixel", bufs=6))
         flip_psum = ctx.enter_context(tc.psum_pool(name="flip", bufs=SIDE))
         y_psum = ctx.enter_context(tc.psum_pool(name="y", bufs=2))
@@ -95,11 +107,11 @@ def tile_iwht3layer_pa_t_e_kernel(tc, trans, weight_words, weight_scales, bias, 
         nc.gpsimd.memset(bias_row[:], 0.0)
         bias_sb = const.tile([P, C_OUT], F32)
 
-        planes_low = const.tile([P, 2 * SIDE * PASSES, C_OUT], U8, align_bytes=64)
-        nc.vector.memset(planes_low[:].bitcast(I32), 0)
-        planes_high = const.tile([P, 2 * SIDE * PASSES, C_OUT], U8, align_bytes=64)
-        nc.vector.memset(planes_high[:].bitcast(I32), 0)
-        w_planes = (planes_low, planes_high)
+        w_planes = []
+        for u in range(SIDE):
+            planes = const.tile([P, SIDE * PASSES, C_OUT], U8, align_bytes=64, name="planes%d" % u)
+            nc.vector.memset(planes[:].bitcast(I32), 0)
+            w_planes.append(planes)
 
         ctx.enter_context(tc.manual_schedule())
 
@@ -111,13 +123,14 @@ def tile_iwht3layer_pa_t_e_kernel(tc, trans, weight_words, weight_scales, bias, 
         y_banks = {}
         stage1_tiles = {}
         stage2_tiles = {}
-        stage3_tiles = {}
+        acc_tiles = {}
+        pixel_tiles = {}
 
-        def load_weight_scales(half):
-            passes = slice(half * 2 * SIDE * PASSES, (half + 1) * 2 * SIDE * PASSES)
+        def load_weight_scales(u):
+            passes = slice(u * SIDE * PASSES, (u + 1) * SIDE * PASSES)
             for r in range(4):
                 nc.sync.dma_start(
-                    out=w_planes[half][r : P : 32, :, :].bitcast(I32),
+                    out=w_planes[u][r : P : 32, :, :].bitcast(I32),
                     in_=weight_scales[passes, r : 16 : 4, :].rearrange("g q n -> q g n").bitcast(I32),
                 )
 
@@ -135,19 +148,20 @@ def tile_iwht3layer_pa_t_e_kernel(tc, trans, weight_words, weight_scales, bias, 
                 nc.sync.dma_start(out=x_raw[:], in_=x_dram[u, v, rt])
                 x_tiles[step].append(x_raw)
 
-        def load_step(step):
-            if step == 0:
-                load_rows(0)
+        def load(token):
+            kind, n = token[0], int(token[1:] or 0)
+            if kind == "x":
+                load_rows(n)
+            elif kind == "s":
+                load_weight_scales(n)
+            elif kind == "w":
+                load_weight_words(n)
+            else:
                 nc.sync.dma_start(out=bias_row[0:1, :], in_=bias.rearrange("a b c k -> (a b c) k"))
-            if step + 1 < STEPS:
-                load_rows(step + 1)
-            rt, u = place(step)
-            if rt == 0:
-                if u % 2 == 0:
-                    load_weight_scales(u // 2)
-                load_weight_words(u)
 
         def warm_up(count):
+            if count == 0:
+                return
             flipped = flip_psum.tile([P, C_IN // 2], F32)
             for i in range(count):
                 nc.tensor.matmul(flipped[:], lhsT=ones[:, 0:P], rhs=ones[:], start=True, stop=True)
@@ -213,13 +227,17 @@ def tile_iwht3layer_pa_t_e_kernel(tc, trans, weight_words, weight_scales, bias, 
                     lhsT=codes[:, rows].bitcast(FP8X4),
                     lhsT_scale=x_scales[:, rows],
                     rhs=w_tiles[u][:, v * PASSES + g, :].bitcast(FP8X4),
-                    rhs_scale=w_planes[u // 2][:, ((u % 2) * SIDE + v) * PASSES + g, :],
+                    rhs_scale=w_planes[u][:, v * PASSES + g, :],
                     start=start,
                     stop=stop,
                 )
 
             left, right = slice(0, C_OUT), slice(C_OUT, 2 * C_OUT)
-            if all_from_psum(step):
+            if scheme(step) == "F":
+                groups = ((bank_a[:, left], (0,)), (bank_a[:, right], (3,)), (bank_b[:, left], (1,)), (bank_b[:, right], (2,)))
+            elif scheme(step) == "E":
+                groups = ((bank_a[:, left], (1, 3)), (bank_a[:, right], (0, 2)), (bank_b[:, left], (2, 3)), (bank_b[:, right], (1, 2)))
+            elif all_from_psum(step):
                 groups = ((bank_a[:, left], (1, 3)), (bank_a[:, right], (0, 1, 2, 3)), (bank_b[:, left], (2, 3)), (bank_b[:, right], (1, 2)))
             else:
                 groups = ((bank_a[:, left], (0, 1)), (bank_a[:, right], (2, 3)), (bank_b[:, left], (1,)), (bank_b[:, right], (3,)))
@@ -229,8 +247,22 @@ def tile_iwht3layer_pa_t_e_kernel(tc, trans, weight_words, weight_scales, bias, 
                         mx_pass(acc, v, g, start=(v == members[0] and g == 0), stop=(v == members[-1] and g == PASSES - 1))
 
         def copy_sums(step):
+            if scheme(step) == "F":
+                stage2_tiles[step] = row_pool.tile([P, SIDE, C_OUT], F32, name="stage2")
+                singles = stage_pool.tile([P, SIDE, C_OUT], F32, name="singles")
+                stage1_tiles[step] = singles
+                nc.scalar.activation(out=singles[:, 3, :], in_=y_banks[step][0][:, C_OUT : 2 * C_OUT], func=COPY, scale=1.0 / 16.0)
+                nc.scalar.activation(out=singles[:, 1, :], in_=y_banks[step][1][:, 0:C_OUT], func=COPY, scale=1.0 / 16.0)
+                return
+            if scheme(step) == "E":
+                stage2_tiles[step] = row_pool.tile([P, SIDE, C_OUT], F32, name="stage2")
+                half_sum = stage_pool.tile([P, C_OUT], F32, name="half")
+                stage1_tiles[step] = half_sum
+                if place(step)[1] != 0:
+                    nc.scalar.activation(out=half_sum[:], in_=y_banks[step][0][:, 0:C_OUT], func=COPY, scale=1.0 / 16.0)
+                return
             if all_from_psum(step):
-                stage2 = stage_pool.tile([P, SIDE, C_OUT], F32)
+                stage2 = row_pool.tile([P, SIDE, C_OUT], F32)
                 stage2_tiles[step] = stage2
                 if place(step)[1] != 0:
                     nc.scalar.activation(out=stage2[:, 0, :], in_=y_banks[step][0][:, C_OUT : 2 * C_OUT], func=COPY, scale=1.0 / 16.0)
@@ -245,7 +277,13 @@ def tile_iwht3layer_pa_t_e_kernel(tc, trans, weight_words, weight_scales, bias, 
             stage1_tiles[step] = stage1
 
         def add_bias(step):
-            if place(step)[1] != 0:
+            if scheme(step) == "E":
+                if place(step)[1] == 0:
+                    nc.vector.scalar_tensor_tensor(
+                        out=stage1_tiles[step][:], in0=y_banks[step][0][:, 0:C_OUT], scalar=1.0 / 16.0, in1=bias_sb[:], op0=MULT, op1=ADD
+                    )
+                return
+            if place(step)[1] != 0 or scheme(step) == "F":
                 return
             if all_from_psum(step):
                 nc.vector.scalar_tensor_tensor(
@@ -262,6 +300,40 @@ def tile_iwht3layer_pa_t_e_kernel(tc, trans, weight_words, weight_scales, bias, 
 
         def differences(step, parts=(0, 1)):
             bank_a, bank_b = y_banks[step]
+            if scheme(step) == "F":
+                stage2, s = stage2_tiles[step], stage1_tiles[step]
+                def stt(out, in0, k, in1, op):
+                    nc.vector.scalar_tensor_tensor(out=out, in0=in0, scalar=k / 16.0, in1=in1, op0=MULT, op1=op)
+                stt(s[:, 2, :], bank_b[:, C_OUT : 2 * C_OUT], 1.0, s[:, 3, :], SUBTRACT)
+                stt(s[:, 0, :], bank_a[:, 0:C_OUT], 1.0, s[:, 1, :], ADD)
+                nc.vector.tensor_tensor(out=s[:, 0, :], in0=s[:, 0, :], in1=s[:, 2, :], op=ADD)
+                w = s[:, 0:1, :]
+                stt(stage2[:, 0, :], bank_a[:, C_OUT : 2 * C_OUT], 2.0, s[:, 0, :], ADD)
+                stt(stage2[:, 1:3, :], bank_b[:].rearrange("p (m k) -> p m k", m=2), -2.0, w.to_broadcast([P, 2, C_OUT]), ADD)
+                stt(stage2[:, 3, :], bank_a[:, 0:C_OUT], 2.0, s[:, 0, :], SUBTRACT)
+                return
+            if scheme(step) == "E":
+                stage2 = stage2_tiles[step]
+                if 0 in parts:
+                    nc.vector.scalar_tensor_tensor(
+                        out=stage2[:, 0, :], in0=bank_a[:, C_OUT : 2 * C_OUT], scalar=1.0 / 16.0, in1=stage1_tiles[step][:], op0=MULT, op1=ADD
+                    )
+                    if SPLITD and parts == (0, 1):
+                        last_written[0] = None
+                        make_waiting(1)
+                    nc.vector.scalar_tensor_tensor(
+                        out=stage2[:, 1, :], in0=bank_a[:, 0:C_OUT], scalar=-2.0 / 16.0, in1=stage2[:, 0, :], op0=MULT, op1=ADD
+                    )
+                if 1 in parts:
+                    nc.vector.scalar_tensor_tensor(
+                        out=stage2[:, 2:4, :],
+                        in0=bank_b[:].rearrange("p (m k) -> p m k", m=2),
+                        scalar=-2.0 / 16.0,
+                        in1=stage2[:, 0:1, :].to_broadcast([P, 2, C_OUT]),
+                        op0=MULT,
+                        op1=ADD,
+                    )
+                return
             if not all_from_psum(step):
                 stage1 = stage1_tiles[step]
                 nc.vector.scalar_tensor_tensor(
@@ -290,70 +362,98 @@ def tile_iwht3layer_pa_t_e_kernel(tc, trans, weight_words, weight_scales, bias, 
 
         def second_butterfly(step):
             stage1 = stage1_tiles[step]
-            stage2 = stage_pool.tile([P, SIDE, C_OUT], F32)
+            stage2 = row_pool.tile([P, SIDE, C_OUT], F32)
             nc.vector.tensor_tensor(out=stage2[:, 0:2, :], in0=stage1[:, 0:2, :], in1=stage1[:, 2:4, :], op=ADD)
             nc.vector.tensor_tensor(out=stage2[:, 2:4, :], in0=stage1[:, 0:2, :], in1=stage1[:, 2:4, :], op=SUBTRACT)
             stage2_tiles[step] = stage2
 
         def row_operation(out_row, in0, in1, op, shared):
-            end = 3 * C_OUT + 8 if shared else ROW_COLS
+            end = ROW_COLS - SHARE + 8 if shared else ROW_COLS
             nc.vector.tensor_tensor(out=out_row[:, 0:end], in0=in0[:, 0:end], in1=in1[:, 0:end], op=op)
             if shared:
-                rest = slice(3 * C_OUT, ROW_COLS)
+                rest = slice(ROW_COLS - SHARE, ROW_COLS)
                 nc.gpsimd.tensor_tensor(out=out_row[:, rest], in0=in0[:, rest], in1=in1[:, rest], op=op)
 
-        def third_butterfly(step, low_p, shared):
-            rt, u = place(step)
-            stage3 = stage3_pool.tile([P, ROW_COLS], F32)
-            row_operation(
-                stage3,
-                stage2_tiles[step - 1][:].rearrange("p q k -> p (q k)"),
-                stage2_tiles[step][:].rearrange("p q k -> p (q k)"),
-                ADD if low_p == 0 else SUBTRACT,
-                shared,
-            )
-            stage3_tiles[(rt, low_p, u // 2)] = stage3
+        step_of = {place(step): step for step in range(STEPS)}
 
-        def last_butterfly(rt, p, shared):
-            pixels = pixel_pool.tile([P, ROW_COLS], F32)
-            row_operation(
-                pixels, stage3_tiles[(rt, p % 2, 0)], stage3_tiles[(rt, p % 2, 1)], ADD if p < 2 else SUBTRACT, shared
+        def row(rt, u, cols):
+            return stage2_tiles[step_of[(rt, u)]][:].rearrange("p q k -> p (q k)")[:, cols]
+
+        ALL = slice(0, ROW_COLS)
+
+        def accumulate(rt, u, shared, cols=ALL):
+            if u == 1 and rt not in acc_tiles:
+                acc = acc_pool.tile([P, ROW_COLS], F32)
+                acc_tiles[rt] = acc
+            acc = acc_tiles[rt]
+            first = row(rt, 0, cols) if u == 1 else acc[:, cols]
+            if cols is ALL:
+                row_operation(acc, row(rt, 0, cols) if u == 1 else acc, row(rt, u, cols), SUBTRACT if u == 3 else ADD, shared)
+            else:
+                nc.vector.tensor_tensor(out=acc[:, cols], in0=first, in1=row(rt, u, cols), op=(SUBTRACT if u == 3 else ADD))
+
+        def pixel_row(rt, p, cols=ALL):
+            if (rt, p) not in pixel_tiles:
+                pixels = pixel_pool.tile([P, ROW_COLS], F32)
+                pixel_tiles[(rt, p)] = pixels
+            pixels = pixel_tiles[(rt, p)]
+            nc.vector.scalar_tensor_tensor(
+                out=pixels[:, cols],
+                in0=row(rt, (3, 1, 2, 0)[p], cols),
+                scalar=(2.0, -2.0, -2.0, 2.0)[p],
+                in1=acc_tiles[rt][:, cols],
+                op0=MULT,
+                op1=(SUBTRACT if p == 3 else ADD),
             )
-            nc.sync.dma_start(out=out_dram[p, rt], in_=pixels[:])
+            nc.sync.dma_start(out=out_dram[p, rt][:, :, cols], in_=pixels[:, cols])
 
         waiting = []
+        last_written = [None]
 
         def enqueue(step):
             rt, u = place(step)
             if not all_from_psum(step):
-                waiting.append(lambda shared: second_butterfly(step))
-            if u % 2 == 1:
-                waiting.append(lambda shared: third_butterfly(step, 0, shared))
-                waiting.append(lambda shared: third_butterfly(step, 1, shared))
+                waiting.append(({("first", step)}, ("row", rt, u), lambda shared: second_butterfly(step)))
+            if u >= 1:
+                reads = {("row", rt, u), ("row", rt, 0) if u == 1 else ("sum", rt)}
+                waiting.append((reads, ("sum", rt), lambda shared: accumulate(rt, u, shared)))
             if u == SIDE - 1:
-                for p in (0, 2, 1, 3):
-                    waiting.append(lambda shared, p=p: last_butterfly(rt, p, shared))
+                for p in (1, 2, 3, 0):
+                    reads = {("row", rt, (3, 1, 2, 0)[p]), ("sum", rt)}
+                    waiting.append((reads, ("pixels", rt, p), lambda shared, p=p: pixel_row(rt, p)))
 
         def make_waiting(limit, shared=False):
-            for operation in waiting[:limit]:
+            for turn in range(min(limit, len(waiting))):
+                best = 0
+                if SKIP:
+                    for index, (reads, writes, operation) in enumerate(waiting):
+                        before = {entry[1] for entry in waiting[:index]}
+                        if last_written[0] not in reads and not before & (reads | {writes}):
+                            best = index
+                            break
+                reads, writes, operation = waiting.pop(best)
                 operation(shared)
-            rest = waiting[limit:]
-            waiting.clear()
-            waiting.extend(rest)
+                last_written[0] = writes
 
-        for step in range(STEPS_LOADED_AHEAD - 1):
-            load_step(step)
+        for token in HEAD.split():
+            load(token)
 
-        warm_up(4)
+        warm_up(WARM0)
         for s in range(-1, STEPS if TAIL else STEPS + 1):
             w0, w1, w2 = waits(s)
-            if s + STEPS_LOADED_AHEAD < STEPS:
-                load_step(s + STEPS_LOADED_AHEAD)
-            if LAG == 3 and s >= 1:
+            if 0 <= s and s + XB < STEPS:
+                load("x%d" % (s + XB))
+            for token in LATER.get(s, "").split():
+                load(token)
+            early = s < EARLY and 0 <= s
+            if early:
+                multiply(s)
+                copy_sums(s)
+            if LAG == 3 and s - 1 >= EARLY:
                 copy_sums(s - 1)
             if s + 1 < STEPS:
                 transpose_and_regroup(s + 1, 0)
-            if LAG == 3 and s >= 1:
+            if LAG == 3 and s - 1 >= EARLY:
                 multiply(s - 1, (1,))
             sorts = sorted_of(s + 2) if s + 2 < STEPS else ()
             if LAG == 3:
@@ -363,27 +463,30 @@ def tile_iwht3layer_pa_t_e_kernel(tc, trans, weight_words, weight_scales, bias, 
                 transpose_and_regroup(s + 1, 1)
             if s == -1:
                 spread_bias()
-                warm_up(2)
+                warm_up(WARM1)
             if LAG == 3:
-                if 0 <= s < STEPS:
+                if 0 <= s < STEPS and not early:
                     multiply(s, (0,))
                 for v in sorts[(len(sorts) + 1) // 2 :]:
                     sort_words(s + 2, v)
             else:
-                if 0 <= s < STEPS:
+                if 0 <= s < STEPS and not early:
                     multiply(s)
                 for v in sorts:
                     sort_words(s + 2, v)
-                if 0 <= s < STEPS:
+                if 0 <= s < STEPS and not early:
                     copy_sums(s)
             if s >= 1:
                 add_bias(s - 1)
-                make_waiting(w0, shared=shared_at(s))
+                last_written[0] = None
+                make_waiting(WB if place(s - 1)[1] == 0 else w0, shared=shared_at(s))
                 differences(s - 1)
+                last_written[0] = ("row",) + place(s - 1) if all_from_psum(s - 1) else ("first", s - 1)
                 enqueue(s - 1)
             make_waiting(w1)
             if s + 1 < STEPS:
                 quantise(s + 1)
+                last_written[0] = None
             make_waiting(w2 if s < STEPS - 1 else len(waiting))
 
         if TAIL:
@@ -392,23 +495,39 @@ def tile_iwht3layer_pa_t_e_kernel(tc, trans, weight_words, weight_scales, bias, 
             if LAG == 3:
                 copy_sums(last)
                 multiply(last, (1,))
-            stage3 = [stage3_pool.tile([P, ROW_COLS], F32, name="stage3") for low_p in range(2)]
-            pixels = [pixel_pool.tile([P, ROW_COLS], F32, name="pixels") for p in range(SIDE)]
+            if TAIL == 3:
+                acc = acc_tiles[rt]
+                partial = {}
+                for p in (1, 2, 3):
+                    partial[p] = row_pool.tile([P, SIDE, C_OUT], F32, name="stage2")
+                    nc.vector.scalar_tensor_tensor(
+                        out=partial[p][:].rearrange("p q k -> p (q k)"), in0=row(rt, (0, 1, 2, 0)[p], ALL), scalar=-2.0, in1=acc[:], op0=MULT, op1=ADD
+                    )
+                pixels = [pixel_pool.tile([P, ROW_COLS], F32, name="pixels") for p in range(SIDE)]
+                for part in range(2):
+                    cols = slice(part * ROW_COLS // 2, (part + 1) * ROW_COLS // 2)
+                    differences(last, (part,))
+                    for p in (1, 2, 3, 0):
+                        r3 = row(rt, 3, cols)
+                        if p == 0:
+                            nc.vector.tensor_tensor(out=pixels[p][:, cols], in0=acc[:, cols], in1=r3, op=ADD)
+                        else:
+                            t = partial[p][:].rearrange("p q k -> p (q k)")[:, cols]
+                            nc.vector.tensor_tensor(out=pixels[p][:, cols], in0=(r3 if p == 3 else t), in1=(t if p == 3 else r3), op=SUBTRACT)
+                        nc.sync.dma_start(out=out_dram[p, rt][:, :, cols], in_=pixels[p][:, cols])
+                return
+            halves = [slice(part * ROW_COLS // 2, (part + 1) * ROW_COLS // 2) for part in range(2)]
+            if TAIL == 4:
+                differences(last)
+                for cols in halves:
+                    accumulate(rt, SIDE - 1, False, cols)
+                for cols in halves:
+                    for p in (1, 2, 3, 0):
+                        pixel_row(rt, p, cols)
+                return
             for part in range(2):
-                cols = slice(part * ROW_COLS // 2, (part + 1) * ROW_COLS // 2)
+                cols = halves[part]
                 differences(last, (part,))
-                for low_p in range(2):
-                    nc.vector.tensor_tensor(
-                        out=stage3[low_p][:, cols],
-                        in0=stage2_tiles[last - 1][:].rearrange("p q k -> p (q k)")[:, cols],
-                        in1=stage2_tiles[last][:].rearrange("p q k -> p (q k)")[:, cols],
-                        op=(ADD if low_p == 0 else SUBTRACT),
-                    )
-                for p in (0, 2, 1, 3):
-                    nc.vector.tensor_tensor(
-                        out=pixels[p][:, cols],
-                        in0=stage3_tiles[(rt, p % 2, 0)][:, cols],
-                        in1=stage3[p % 2][:, cols],
-                        op=(ADD if p < 2 else SUBTRACT),
-                    )
-                    nc.sync.dma_start(out=out_dram[p, rt][:, :, cols], in_=pixels[p][:, cols])
+                accumulate(rt, SIDE - 1, False, cols)
+                for p in (1, 2, 3, 0):
+                    pixel_row(rt, p, cols)

@@ -42,15 +42,15 @@ TAIL = 4
 
 
 def scheme(step):
-    return "PPPPPQQQQQQQQQQQ"[step]
+    return "PPPPPPQQQQQQQQQQ"[step]
 
 
 def sorted_of(step):
-    return () if step < 2 else (0,)
+    return () if step < 2 else (0, 1, 2) if scheme(step) == "Q" else (0, 2)
 
 
 def waits(s):
-    return (1, 1, 0)
+    return (0, 1, 1)
 
 
 def vevac(step):
@@ -87,7 +87,7 @@ def tile_iwht3layer_pa_t_e_kernel(tc, trans, weight_words, weight_scales, bias, 
         const = ctx.enter_context(tc.tile_pool(name="const", bufs=1))
         w_pool = ctx.enter_context(tc.tile_pool(name="w", bufs=SIDE))
         x_pool = ctx.enter_context(tc.tile_pool(name="x", bufs=XB * SIDE))
-        sorted_pool = ctx.enter_context(tc.tile_pool(name="sorted", bufs=4))
+        sorted_pool = ctx.enter_context(tc.tile_pool(name="sorted", bufs=6))
         quant_pool = ctx.enter_context(tc.tile_pool(name="quant", bufs=3))
         stage_pool = ctx.enter_context(tc.tile_pool(name="stage", bufs=4))
         row_pool = ctx.enter_context(tc.tile_pool(name="row", bufs=R2B))

@@ -27,22 +27,26 @@ STEPS_LOADED_AHEAD = 3
 LAG = 2
 SPLITD = False
 SKIP = True
+XBIG = 16
+LONG = 99
+WLONG = (1, 1, 1)
 WB = 1
 WARM0 = 4
 WARM1 = 2
-ORDER = ((0, 0), (1, 0), (0, 1), (1, 1), (2, 0), (2, 1), (3, 0), (3, 1))
+ORDER = tuple((rt, u) for u in range(4) for rt in (0, 1)) + tuple((rt, u) for rt in (2, 3) for u in range(4))
 R2B = 10
-ACCB = 3
+ACCB = 4
+PIXB = 5
 XB = 4
 EARLY = 0
-HEAD = "x0 b x1 s0 w0 x2 s1 w1 x3"
-LATER = {1: "s2 w2", 2: "s3 w3"}
+HEAD = "x0 b x1 s0 w0 x2 x3 s1 w1"
+LATER = {1: "s2 w2", 3: "s3 w3"}
 SHARE = 256
 TAIL = 4
 
 
 def scheme(step):
-    return "PPPPPPQQQQQQQQQQ"[step]
+    return "PPPPPPEEQQQQQQQQ"[step]
 
 
 def sorted_of(step):
@@ -67,6 +71,8 @@ FLOPS = 2 * SIDE * SIDE * ROW_TILES * P * C_IN * C_OUT
 
 
 def place(step):
+    if len(ORDER) == STEPS:
+        return ORDER[step]
     pair, u_low = divmod(step, 2)
     rt, u_high = ORDER[pair]
     return rt, 2 * u_high + u_low
@@ -86,13 +92,13 @@ def tile_iwht3layer_pa_t_e_kernel(tc, trans, weight_words, weight_scales, bias, 
     with ExitStack() as ctx:
         const = ctx.enter_context(tc.tile_pool(name="const", bufs=1))
         w_pool = ctx.enter_context(tc.tile_pool(name="w", bufs=SIDE))
-        x_pool = ctx.enter_context(tc.tile_pool(name="x", bufs=XB * SIDE))
+        x_pool = ctx.enter_context(tc.tile_pool(name="x", bufs=XB))
         sorted_pool = ctx.enter_context(tc.tile_pool(name="sorted", bufs=6))
         quant_pool = ctx.enter_context(tc.tile_pool(name="quant", bufs=3))
         stage_pool = ctx.enter_context(tc.tile_pool(name="stage", bufs=4))
         row_pool = ctx.enter_context(tc.tile_pool(name="row", bufs=R2B))
         acc_pool = ctx.enter_context(tc.tile_pool(name="acc", bufs=ACCB))
-        pixel_pool = ctx.enter_context(tc.tile_pool(name="pixel", bufs=6))
+        pixel_pool = ctx.enter_context(tc.tile_pool(name="pixel", bufs=PIXB))
         flip_psum = ctx.enter_context(tc.psum_pool(name="flip", bufs=SIDE))
         y_psum = ctx.enter_context(tc.psum_pool(name="y", bufs=2))
 
@@ -142,11 +148,13 @@ def tile_iwht3layer_pa_t_e_kernel(tc, trans, weight_words, weight_scales, bias, 
 
         def load_rows(step):
             rt, u = place(step)
-            x_tiles[step] = []
-            for v in range(SIDE):
-                x_raw = x_pool.tile([P, C_IN], BF16)
-                nc.sync.dma_start(out=x_raw[:], in_=x_dram[u, v, rt])
-                x_tiles[step].append(x_raw)
+            x_raw = x_pool.tile([P, SIDE, C_IN], BF16)
+            x_tiles[step] = [x_raw[:, v, :] for v in range(SIDE)]
+            if step >= XBIG:
+                nc.sync.dma_start(out=x_raw[:], in_=x_dram[u, :, rt].rearrange("v p c -> p v c"))
+            else:
+                for v in range(SIDE):
+                    nc.sync.dma_start(out=x_raw[:, v, :], in_=x_dram[u, v, rt])
 
         def load(token):
             kind, n = token[0], int(token[1:] or 0)
@@ -175,7 +183,7 @@ def tile_iwht3layer_pa_t_e_kernel(tc, trans, weight_words, weight_scales, bias, 
             x_sorted = sorted_pool.tile([P, C_IN], BF16)
             nc.scalar.copy(
                 out=x_sorted[:].bitcast(F32).rearrange("p (g w j) -> p g w j", g=PASSES, w=2),
-                in_=x_tiles[step][v][:].bitcast(F32).rearrange("p (g j w) -> p g w j", g=PASSES, w=2),
+                in_=x_tiles[step][v].bitcast(F32).rearrange("p (g j w) -> p g w j", g=PASSES, w=2),
             )
             sorted_tiles[(step, v)] = x_sorted
 
@@ -185,7 +193,7 @@ def tile_iwht3layer_pa_t_e_kernel(tc, trans, weight_words, weight_scales, bias, 
                 grouped_tiles[step] = grouped
             for v in (2 * m, 2 * m + 1):
                 is_sorted = (step, v) in sorted_tiles
-                x_words = (sorted_tiles[(step, v)] if is_sorted else x_tiles[step][v])[:].bitcast(F32)
+                x_words = (sorted_tiles[(step, v)][:] if is_sorted else x_tiles[step][v]).bitcast(F32)
                 flipped = flip_psum.tile([P, C_IN // 2], F32)
                 for g in range(PASSES):
                     for w in range(2):
@@ -368,7 +376,10 @@ def tile_iwht3layer_pa_t_e_kernel(tc, trans, weight_words, weight_scales, bias, 
             stage2_tiles[step] = stage2
 
         def row_operation(out_row, in0, in1, op, shared):
-            end = ROW_COLS - SHARE + 8 if shared else ROW_COLS
+            if not shared:
+                nc.vector.tensor_tensor(out=out_row, in0=in0, in1=in1, op=op)
+                return
+            end = ROW_COLS - SHARE + 8
             nc.vector.tensor_tensor(out=out_row[:, 0:end], in0=in0[:, 0:end], in1=in1[:, 0:end], op=op)
             if shared:
                 rest = slice(ROW_COLS - SHARE, ROW_COLS)
@@ -382,15 +393,11 @@ def tile_iwht3layer_pa_t_e_kernel(tc, trans, weight_words, weight_scales, bias, 
         ALL = slice(0, ROW_COLS)
 
         def accumulate(rt, u, shared, cols=ALL):
-            if u == 1 and rt not in acc_tiles:
+            first = row(rt, 0, cols) if u == 1 else acc_tiles[(rt, u - 1)][:, cols]
+            if (rt, u) not in acc_tiles:
                 acc = acc_pool.tile([P, ROW_COLS], F32)
-                acc_tiles[rt] = acc
-            acc = acc_tiles[rt]
-            first = row(rt, 0, cols) if u == 1 else acc[:, cols]
-            if cols is ALL:
-                row_operation(acc, row(rt, 0, cols) if u == 1 else acc, row(rt, u, cols), SUBTRACT if u == 3 else ADD, shared)
-            else:
-                nc.vector.tensor_tensor(out=acc[:, cols], in0=first, in1=row(rt, u, cols), op=(SUBTRACT if u == 3 else ADD))
+                acc_tiles[(rt, u)] = acc
+            row_operation(acc_tiles[(rt, u)][:, cols], first, row(rt, u, cols), SUBTRACT if u == 3 else ADD, shared)
 
         def pixel_row(rt, p, cols=ALL):
             if (rt, p) not in pixel_tiles:
@@ -401,7 +408,7 @@ def tile_iwht3layer_pa_t_e_kernel(tc, trans, weight_words, weight_scales, bias, 
                 out=pixels[:, cols],
                 in0=row(rt, (3, 1, 2, 0)[p], cols),
                 scalar=(2.0, -2.0, -2.0, 2.0)[p],
-                in1=acc_tiles[rt][:, cols],
+                in1=acc_tiles[(rt, SIDE - 1)][:, cols],
                 op0=MULT,
                 op1=(SUBTRACT if p == 3 else ADD),
             )
@@ -440,7 +447,7 @@ def tile_iwht3layer_pa_t_e_kernel(tc, trans, weight_words, weight_scales, bias, 
 
         warm_up(WARM0)
         for s in range(-1, STEPS if TAIL else STEPS + 1):
-            w0, w1, w2 = waits(s)
+            w0, w1, w2 = waits(s) if len(waiting) < LONG else WLONG
             if 0 <= s and s + XB < STEPS:
                 load("x%d" % (s + XB))
             for token in LATER.get(s, "").split():
@@ -496,7 +503,7 @@ def tile_iwht3layer_pa_t_e_kernel(tc, trans, weight_words, weight_scales, bias, 
                 copy_sums(last)
                 multiply(last, (1,))
             if TAIL == 3:
-                acc = acc_tiles[rt]
+                acc = acc_tiles[(rt, 2)]
                 partial = {}
                 for p in (1, 2, 3):
                     partial[p] = row_pool.tile([P, SIDE, C_OUT], F32, name="stage2")
@@ -504,9 +511,9 @@ def tile_iwht3layer_pa_t_e_kernel(tc, trans, weight_words, weight_scales, bias, 
                         out=partial[p][:].rearrange("p q k -> p (q k)"), in0=row(rt, (0, 1, 2, 0)[p], ALL), scalar=-2.0, in1=acc[:], op0=MULT, op1=ADD
                     )
                 pixels = [pixel_pool.tile([P, ROW_COLS], F32, name="pixels") for p in range(SIDE)]
+                differences(last)
                 for part in range(2):
                     cols = slice(part * ROW_COLS // 2, (part + 1) * ROW_COLS // 2)
-                    differences(last, (part,))
                     for p in (1, 2, 3, 0):
                         r3 = row(rt, 3, cols)
                         if p == 0:

from contextlib import ExitStack

import concourse.mybir as mybir
from concourse.masks import make_identity

F32 = mybir.dt.float32
BF16 = mybir.dt.bfloat16
I32 = mybir.dt.int32
U32 = mybir.dt.uint32
U8 = mybir.dt.uint8
FP8X4 = mybir.dt.float8_e4m3fn_x4
ADD = mybir.AluOpType.add
SUBTRACT = mybir.AluOpType.subtract
MULT = mybir.AluOpType.mult
COPY = mybir.ActivationFunctionType.Copy

P = 128
SIDE = 4
C_IN = 1024
C_OUT = 256
K_PASS = 4 * P
PASSES = C_IN // K_PASS
ROW_TILES = 4
STEPS = ROW_TILES * SIDE
STEPS_OF_A_HALF = STEPS // 2
STEPS_LOADED_AHEAD = 3
LAG = 2
SPLITD = False
SKIP = True
XBIG = 16
LONG = 99
WLONG = (1, 1, 1)
WB = 1
WARM0 = 4
WARM1 = 2
ORDER = tuple((rt, u) for u in range(4) for rt in (0, 1)) + tuple((rt, u) for rt in (2, 3) for u in range(4))
R2B = 10
ACCB = 4
PIXB = 5
XB = 4
EARLY = 0
HEAD = "x0 b x1 s0 w0 x2 x3 s1 w1"
LATER = {1: "s2 w2", 3: "s3 w3"}
SHARE = 256
TAIL = 4


def scheme(step):
    return "PPPPPPEEQQQQQQQQ"[step]


def sorted_of(step):
    return () if step < 2 else (0, 1, 2) if scheme(step) == "Q" else (0, 2)


def waits(s):
    return (0, 1, 1)


def vevac(step):
    return ()


def shared_at(s):
    return False


ROW_COLS = SIDE * C_OUT

FLOPS = 2 * SIDE * SIDE * ROW_TILES * P * C_IN * C_OUT


def place(step):
    if len(ORDER) == STEPS:
        return ORDER[step]
    pair, u_low = divmod(step, 2)
    rt, u_high = ORDER[pair]
    return rt, 2 * u_high + u_low


def all_from_psum(step):
    return scheme(step) != "P"


def tile_iwht3layer_pa_t_e_kernel(tc, trans, weight_words, weight_scales, bias, out):
    nc = tc.nc

    x_dram = trans.rearrange("(u v) b i (jj rt) c -> u v rt (b i jj) c", v=SIDE, rt=ROW_TILES)
    out_dram = out.rearrange("b (i p) (jj rt q) k -> p rt (b i) jj (q k)", p=SIDE, rt=ROW_TILES, q=SIDE)
    w_dram = weight_words.rearrange("g p n t -> p g (n t)")

    with ExitStack() as ctx:
        const = ctx.enter_context(tc.tile_pool(name="const", bufs=1))
        w_pool = ctx.enter_context(tc.tile_pool(name="w", bufs=SIDE))
        x_pool = ctx.enter_context(tc.tile_pool(name="x", bufs=XB))
        sorted_pool = ctx.enter_context(tc.tile_pool(name="sorted", bufs=6))
        quant_pool = ctx.enter_context(tc.tile_pool(name="quant", bufs=3))
        stage_pool = ctx.enter_context(tc.tile_pool(name="stage", bufs=4))
        row_pool = ctx.enter_context(tc.tile_pool(name="row", bufs=R2B))
        acc_pool = ctx.enter_context(tc.tile_pool(name="acc", bufs=ACCB))
        pixel_pool = ctx.enter_context(tc.tile_pool(name="pixel", bufs=PIXB))
        flip_psum = ctx.enter_context(tc.psum_pool(name="flip", bufs=SIDE))
        y_psum = ctx.enter_context(tc.psum_pool(name="y", bufs=2))

        ident = const.tile([P, P], F32)
        make_identity(nc, ident[:])

        ones = const.tile([P, 4 * P], BF16)
        nc.gpsimd.memset(ones[:], 1.0)
        table_warmer = const.tile([P, 1], F32)
        nc.scalar.activation(out=table_warmer[:], in_=ones[:, 0:1], func=COPY, scale=1.0 / 16.0)
        bias_row = const.tile([P, C_OUT], BF16)
        nc.gpsimd.memset(bias_row[:], 0.0)
        bias_sb = const.tile([P, C_OUT], F32)

        w_planes = []
        for u in range(SIDE):
            planes = const.tile([P, SIDE * PASSES, C_OUT], U8, align_bytes=64, name="planes%d" % u)
            nc.vector.memset(planes[:].bitcast(I32), 0)
            w_planes.append(planes)

        ctx.enter_context(tc.manual_schedule())

        x_tiles = {}
        sorted_tiles = {}
        w_tiles = {}
        grouped_tiles = {}
        code_tiles = {}
        y_banks = {}
        stage1_tiles = {}
        stage2_tiles = {}
        acc_tiles = {}
        pixel_tiles = {}

        def load_weight_scales(u):
            passes = slice(u * SIDE * PASSES, (u + 1) * SIDE * PASSES)
            for r in range(4):
                nc.sync.dma_start(
                    out=w_planes[u][r : P : 32, :, :].bitcast(I32),
                    in_=weight_scales[passes, r : 16 : 4, :].rearrange("g q n -> q g n").bitcast(I32),
                )

        def load_weight_words(u):
            w_words = w_pool.tile([P, SIDE * PASSES, C_OUT], U32, align_bytes=64)
            first = u * SIDE * PASSES
            nc.sync.dma_start(out=w_words[:].bitcast(I32), in_=w_dram[:, first : first + SIDE * PASSES, :].bitcast(I32))
            w_tiles[u] = w_words

        def load_rows(step):
            rt, u = place(step)
            x_raw = x_pool.tile([P, SIDE, C_IN], BF16)
            x_tiles[step] = [x_raw[:, v, :] for v in range(SIDE)]
            if step >= XBIG:
                nc.sync.dma_start(out=x_raw[:], in_=x_dram[u, :, rt].rearrange("v p c -> p v c"))
            else:
                for v in range(SIDE):
                    nc.sync.dma_start(out=x_raw[:, v, :], in_=x_dram[u, v, rt])

        def load(token):
            kind, n = token[0], int(token[1:] or 0)
            if kind == "x":
                load_rows(n)
            elif kind == "s":
                load_weight_scales(n)
            elif kind == "w":
                load_weight_words(n)
            else:
                nc.sync.dma_start(out=bias_row[0:1, :], in_=bias.rearrange("a b c k -> (a b c) k"))

        def warm_up(count):
            if count == 0:
                return
            flipped = flip_psum.tile([P, C_IN // 2], F32)
            for i in range(count):
                nc.tensor.matmul(flipped[:], lhsT=ones[:, 0:P], rhs=ones[:], start=True, stop=True)

        def spread_bias():
            flipped = flip_psum.tile([P, C_IN // 2], F32)
            nc.tensor.matmul(flipped[:, 0:C_OUT], lhsT=ones[:, 0:P], rhs=bias_row[:], start=True, stop=True)
            nc.scalar.copy(out=bias_sb[:], in_=flipped[:, 0:C_OUT])

        def sort_words(step, v):
            x_sorted = sorted_pool.tile([P, C_IN], BF16)
            nc.scalar.copy(
                out=x_sorted[:].bitcast(F32).rearrange("p (g w j) -> p g w j", g=PASSES, w=2),
                in_=x_tiles[step][v].bitcast(F32).rearrange("p (g j w) -> p g w j", g=PASSES, w=2),
            )
            sorted_tiles[(step, v)] = x_sorted

        def transpose_and_regroup(step, m):
            if m == 0:
                grouped = quant_pool.tile([P, SIDE * C_IN], BF16, align_bytes=64)
                grouped_tiles[step] = grouped
            for v in (2 * m, 2 * m + 1):
                is_sorted = (step, v) in sorted_tiles
                x_words = (sorted_tiles[(step, v)][:] if is_sorted else x_tiles[step][v]).bitcast(F32)
                flipped = flip_psum.tile([P, C_IN // 2], F32)
                for g in range(PASSES):
                    for w in range(2):
                        nc.tensor.transpose(
                            flipped[:, (2 * g + w) * P : (2 * g + w + 1) * P],
                            (
                                x_words[:, (2 * g + w) * P : (2 * g + w + 1) * P]
                                if is_sorted
                                else x_words[:, (K_PASS // 2) * g + w : (K_PASS // 2) * (g + 1) : 2]
                            ),
                            ident[:],
                        )
                (nc.vector.tensor_copy if v in vevac(step) else nc.scalar.copy)(
                    out=grouped_tiles[step][:, v * C_IN : (v + 1) * C_IN]
                    .bitcast(F32)
                    .rearrange("p (g r w) -> p g r w", g=PASSES, w=2),
                    in_=flipped[:].rearrange("p (g w r) -> p g r w", g=PASSES, w=2),
                )

        def quantise(step):
            codes = quant_pool.tile([P, SIDE * PASSES * P], U32, align_bytes=64)
            x_scales = quant_pool.tile([P, SIDE * PASSES * P], U8, align_bytes=64)
            nc.vector.quantize_mx(out=codes[:].bitcast(FP8X4), scales=x_scales[:], in_=grouped_tiles[step][:])
            code_tiles[step] = (codes, x_scales)

        def multiply(step, halves=(0, 1)):
            u = place(step)[1]
            codes, x_scales = code_tiles[step]
            if 0 in halves:
                bank_a = y_psum.tile([P, 2 * C_OUT], F32)
                bank_b = y_psum.tile([P, 2 * C_OUT], F32)
                y_banks[step] = (bank_a, bank_b)
            bank_a, bank_b = y_banks[step]

            def mx_pass(acc, v, g, start, stop):
                rows = slice((v * PASSES + g) * P, (v * PASSES + g + 1) * P)
                nc.tensor.matmul_mx(
                    out=acc,
                    lhsT=codes[:, rows].bitcast(FP8X4),
                    lhsT_scale=x_scales[:, rows],
                    rhs=w_tiles[u][:, v * PASSES + g, :].bitcast(FP8X4),
                    rhs_scale=w_planes[u][:, v * PASSES + g, :],
                    start=start,
                    stop=stop,
                )

            left, right = slice(0, C_OUT), slice(C_OUT, 2 * C_OUT)
            if scheme(step) == "F":
                groups = ((bank_a[:, left], (0,)), (bank_a[:, right], (3,)), (bank_b[:, left], (1,)), (bank_b[:, right], (2,)))
            elif scheme(step) == "E":
                groups = ((bank_a[:, left], (1, 3)), (bank_a[:, right], (0, 2)), (bank_b[:, left], (2, 3)), (bank_b[:, right], (1, 2)))
            elif all_from_psum(step):
                groups = ((bank_a[:, left], (1, 3)), (bank_a[:, right], (0, 1, 2, 3)), (bank_b[:, left], (2, 3)), (bank_b[:, right], (1, 2)))
            else:
                groups = ((bank_a[:, left], (0, 1)), (bank_a[:, right], (2, 3)), (bank_b[:, left], (1,)), (bank_b[:, right], (3,)))
            for acc, members in groups[2 * halves[0] : 2 * halves[-1] + 2]:
                for v in members:
                    for g in range(PASSES):
                        mx_pass(acc, v, g, start=(v == members[0] and g == 0), stop=(v == members[-1] and g == PASSES - 1))

        def copy_sums(step):
            if scheme(step) == "F":
                stage2_tiles[step] = row_pool.tile([P, SIDE, C_OUT], F32, name="stage2")
                singles = stage_pool.tile([P, SIDE, C_OUT], F32, name="singles")
                stage1_tiles[step] = singles
                nc.scalar.activation(out=singles[:, 3, :], in_=y_banks[step][0][:, C_OUT : 2 * C_OUT], func=COPY, scale=1.0 / 16.0)
                nc.scalar.activation(out=singles[:, 1, :], in_=y_banks[step][1][:, 0:C_OUT], func=COPY, scale=1.0 / 16.0)
                return
            if scheme(step) == "E":
                stage2_tiles[step] = row_pool.tile([P, SIDE, C_OUT], F32, name="stage2")
                half_sum = stage_pool.tile([P, C_OUT], F32, name="half")
                stage1_tiles[step] = half_sum
                if place(step)[1] != 0:
                    nc.scalar.activation(out=half_sum[:], in_=y_banks[step][0][:, 0:C_OUT], func=COPY, scale=1.0 / 16.0)
                return
            if all_from_psum(step):
                stage2 = row_pool.tile([P, SIDE, C_OUT], F32)
                stage2_tiles[step] = stage2
                if place(step)[1] != 0:
                    nc.scalar.activation(out=stage2[:, 0, :], in_=y_banks[step][0][:, C_OUT : 2 * C_OUT], func=COPY, scale=1.0 / 16.0)
                return
            stage1 = stage_pool.tile([P, SIDE, C_OUT], F32)
            nc.scalar.activation(
                out=stage1[:, 0:SIDE:2, :],
                in_=y_banks[step][0][:].rearrange("p (m k) -> p m k", m=2),
                func=COPY,
                scale=1.0 / 16.0,
            )
            stage1_tiles[step] = stage1

        def add_bias(step):
            if scheme(step) == "E":
                if place(step)[1] == 0:
                    nc.vector.scalar_tensor_tensor(
                        out=stage1_tiles[step][:], in0=y_banks[step][0][:, 0:C_OUT], scalar=1.0 / 16.0, in1=bias_sb[:], op0=MULT, op1=ADD
                    )
                return
            if place(step)[1] != 0 or scheme(step) == "F":
                return
            if all_from_psum(step):
                nc.vector.scalar_tensor_tensor(
                    out=stage2_tiles[step][:, 0, :],
                    in0=y_banks[step][0][:, C_OUT : 2 * C_OUT],
                    scalar=1.0 / 16.0,
                    in1=bias_sb[:],
                    op0=MULT,
                    op1=ADD,
                )
            else:
                stage1 = stage1_tiles[step]
                nc.vector.tensor_tensor(out=stage1[:, 0, :], in0=stage1[:, 0, :], in1=bias_sb[:], op=ADD)

        def differences(step, parts=(0, 1)):
            bank_a, bank_b = y_banks[step]
            if scheme(step) == "F":
                stage2, s = stage2_tiles[step], stage1_tiles[step]
                def stt(out, in0, k, in1, op):
                    nc.vector.scalar_tensor_tensor(out=out, in0=in0, scalar=k / 16.0, in1=in1, op0=MULT, op1=op)
                stt(s[:, 2, :], bank_b[:, C_OUT : 2 * C_OUT], 1.0, s[:, 3, :], SUBTRACT)
                stt(s[:, 0, :], bank_a[:, 0:C_OUT], 1.0, s[:, 1, :], ADD)
                nc.vector.tensor_tensor(out=s[:, 0, :], in0=s[:, 0, :], in1=s[:, 2, :], op=ADD)
                w = s[:, 0:1, :]
                stt(stage2[:, 0, :], bank_a[:, C_OUT : 2 * C_OUT], 2.0, s[:, 0, :], ADD)
                stt(stage2[:, 1:3, :], bank_b[:].rearrange("p (m k) -> p m k", m=2), -2.0, w.to_broadcast([P, 2, C_OUT]), ADD)
                stt(stage2[:, 3, :], bank_a[:, 0:C_OUT], 2.0, s[:, 0, :], SUBTRACT)
                return
            if scheme(step) == "E":
                stage2 = stage2_tiles[step]
                if 0 in parts:
                    nc.vector.scalar_tensor_tensor(
                        out=stage2[:, 0, :], in0=bank_a[:, C_OUT : 2 * C_OUT], scalar=1.0 / 16.0, in1=stage1_tiles[step][:], op0=MULT, op1=ADD
                    )
                    if SPLITD and parts == (0, 1):
                        last_written[0] = None
                        make_waiting(1)
                    nc.vector.scalar_tensor_tensor(
                        out=stage2[:, 1, :], in0=bank_a[:, 0:C_OUT], scalar=-2.0 / 16.0, in1=stage2[:, 0, :], op0=MULT, op1=ADD
                    )
                if 1 in parts:
                    nc.vector.scalar_tensor_tensor(
                        out=stage2[:, 2:4, :],
                        in0=bank_b[:].rearrange("p (m k) -> p m k", m=2),
                        scalar=-2.0 / 16.0,
                        in1=stage2[:, 0:1, :].to_broadcast([P, 2, C_OUT]),
                        op0=MULT,
                        op1=ADD,
                    )
                return
            if not all_from_psum(step):
                stage1 = stage1_tiles[step]
                nc.vector.scalar_tensor_tensor(
                    out=stage1[:, 1:SIDE:2, :],
                    in0=bank_b[:].rearrange("p (m k) -> p m k", m=2),
                    scalar=-2.0 / 16.0,
                    in1=stage1[:, 0:SIDE:2, :],
                    op0=MULT,
                    op1=ADD,
                )
                return
            stage2 = stage2_tiles[step]
            if 0 in parts:
                nc.vector.scalar_tensor_tensor(
                    out=stage2[:, 1, :], in0=bank_a[:, 0:C_OUT], scalar=-2.0 / 16.0, in1=stage2[:, 0, :], op0=MULT, op1=ADD
                )
            if 1 in parts:
                nc.vector.scalar_tensor_tensor(
                    out=stage2[:, 2:4, :],
                    in0=bank_b[:].rearrange("p (m k) -> p m k", m=2),
                    scalar=-2.0 / 16.0,
                    in1=stage2[:, 0:1, :].to_broadcast([P, 2, C_OUT]),
                    op0=MULT,
                    op1=ADD,
                )

        def second_butterfly(step):
            stage1 = stage1_tiles[step]
            stage2 = row_pool.tile([P, SIDE, C_OUT], F32)
            nc.vector.tensor_tensor(out=stage2[:, 0:2, :], in0=stage1[:, 0:2, :], in1=stage1[:, 2:4, :], op=ADD)
            nc.vector.tensor_tensor(out=stage2[:, 2:4, :], in0=stage1[:, 0:2, :], in1=stage1[:, 2:4, :], op=SUBTRACT)
            stage2_tiles[step] = stage2

        def row_operation(out_row, in0, in1, op, shared):
            if not shared:
                nc.vector.tensor_tensor(out=out_row, in0=in0, in1=in1, op=op)
                return
            end = ROW_COLS - SHARE + 8
            nc.vector.tensor_tensor(out=out_row[:, 0:end], in0=in0[:, 0:end], in1=in1[:, 0:end], op=op)
            if shared:
                rest = slice(ROW_COLS - SHARE, ROW_COLS)
                nc.gpsimd.tensor_tensor(out=out_row[:, rest], in0=in0[:, rest], in1=in1[:, rest], op=op)

        step_of = {place(step): step for step in range(STEPS)}

        def row(rt, u, cols):
            return stage2_tiles[step_of[(rt, u)]][:].rearrange("p q k -> p (q k)")[:, cols]

        ALL = slice(0, ROW_COLS)

        def accumulate(rt, u, shared, cols=ALL):
            first = row(rt, 0, cols) if u == 1 else acc_tiles[(rt, u - 1)][:, cols]
            if (rt, u) not in acc_tiles:
                acc = acc_pool.tile([P, ROW_COLS], F32)
                acc_tiles[(rt, u)] = acc
            row_operation(acc_tiles[(rt, u)][:, cols], first, row(rt, u, cols), SUBTRACT if u == 3 else ADD, shared)

        def pixel_row(rt, p, cols=ALL):
            if (rt, p) not in pixel_tiles:
                pixels = pixel_pool.tile([P, ROW_COLS], F32)
                pixel_tiles[(rt, p)] = pixels
            pixels = pixel_tiles[(rt, p)]
            nc.vector.scalar_tensor_tensor(
                out=pixels[:, cols],
                in0=row(rt, (3, 1, 2, 0)[p], cols),
                scalar=(2.0, -2.0, -2.0, 2.0)[p],
                in1=acc_tiles[(rt, SIDE - 1)][:, cols],
                op0=MULT,
                op1=(SUBTRACT if p == 3 else ADD),
            )
            nc.sync.dma_start(out=out_dram[p, rt][:, :, cols], in_=pixels[:, cols])

        waiting = []
        last_written = [None]

        def enqueue(step):
            rt, u = place(step)
            if not all_from_psum(step):
                waiting.append(({("first", step)}, ("row", rt, u), lambda shared: second_butterfly(step)))
            if u >= 1:
                reads = {("row", rt, u), ("row", rt, 0) if u == 1 else ("sum", rt)}
                waiting.append((reads, ("sum", rt), lambda shared: accumulate(rt, u, shared)))
            if u == SIDE - 1:
                for p in (1, 2, 3, 0):
                    reads = {("row", rt, (3, 1, 2, 0)[p]), ("sum", rt)}
                    waiting.append((reads, ("pixels", rt, p), lambda shared, p=p: pixel_row(rt, p)))

        def make_waiting(limit, shared=False):
            for turn in range(min(limit, len(waiting))):
                best = 0
                if SKIP:
                    for index, (reads, writes, operation) in enumerate(waiting):
                        before = {entry[1] for entry in waiting[:index]}
                        if last_written[0] not in reads and not before & (reads | {writes}):
                            best = index
                            break
                reads, writes, operation = waiting.pop(best)
                operation(shared)
                last_written[0] = writes

        for token in HEAD.split():
            load(token)

        warm_up(WARM0)
        for s in range(-1, STEPS if TAIL else STEPS + 1):
            w0, w1, w2 = waits(s) if len(waiting) < LONG else WLONG
            if 0 <= s and s + XB < STEPS:
                load("x%d" % (s + XB))
            for token in LATER.get(s, "").split():
                load(token)
            early = s < EARLY and 0 <= s
            if early:
                multiply(s)
                copy_sums(s)
            if LAG == 3 and s - 1 >= EARLY:
                copy_sums(s - 1)
            if s + 1 < STEPS:
                transpose_and_regroup(s + 1, 0)
            if LAG == 3 and s - 1 >= EARLY:
                multiply(s - 1, (1,))
            sorts = sorted_of(s + 2) if s + 2 < STEPS else ()
            if LAG == 3:
                for v in sorts[: (len(sorts) + 1) // 2]:
                    sort_words(s + 2, v)
            if s + 1 < STEPS:
                transpose_and_regroup(s + 1, 1)
            if s == -1:
                spread_bias()
                warm_up(WARM1)
            if LAG == 3:
                if 0 <= s < STEPS and not early:
                    multiply(s, (0,))
                for v in sorts[(len(sorts) + 1) // 2 :]:
                    sort_words(s + 2, v)
            else:
                if 0 <= s < STEPS and not early:
                    multiply(s)
                for v in sorts:
                    sort_words(s + 2, v)
                if 0 <= s < STEPS and not early:
                    copy_sums(s)
            if s >= 1:
                add_bias(s - 1)
                last_written[0] = None
                make_waiting(WB if place(s - 1)[1] == 0 else w0, shared=shared_at(s))
                differences(s - 1)
                last_written[0] = ("row",) + place(s - 1) if all_from_psum(s - 1) else ("first", s - 1)
                enqueue(s - 1)
            make_waiting(w1)
            if s + 1 < STEPS:
                quantise(s + 1)
                last_written[0] = None
            make_waiting(w2 if s < STEPS - 1 else len(waiting))

        if TAIL:
            last = STEPS - 1
            rt = place(last)[0]
            if LAG == 3:
                copy_sums(last)
                multiply(last, (1,))
            if TAIL == 3:
                acc = acc_tiles[(rt, 2)]
                partial = {}
                for p in (1, 2, 3):
                    partial[p] = row_pool.tile([P, SIDE, C_OUT], F32, name="stage2")
                    nc.vector.scalar_tensor_tensor(
                        out=partial[p][:].rearrange("p q k -> p (q k)"), in0=row(rt, (0, 1, 2, 0)[p], ALL), scalar=-2.0, in1=acc[:], op0=MULT, op1=ADD
                    )
                pixels = [pixel_pool.tile([P, ROW_COLS], F32, name="pixels") for p in range(SIDE)]
                differences(last)
                for part in range(2):
                    cols = slice(part * ROW_COLS // 2, (part + 1) * ROW_COLS // 2)
                    for p in (1, 2, 3, 0):
                        r3 = row(rt, 3, cols)
                        if p == 0:
                            nc.vector.tensor_tensor(out=pixels[p][:, cols], in0=acc[:, cols], in1=r3, op=ADD)
                        else:
                            t = partial[p][:].rearrange("p q k -> p (q k)")[:, cols]
                            nc.vector.tensor_tensor(out=pixels[p][:, cols], in0=(r3 if p == 3 else t), in1=(t if p == 3 else r3), op=SUBTRACT)
                        nc.sync.dma_start(out=out_dram[p, rt][:, :, cols], in_=pixels[p][:, cols])
                return
            halves = [slice(part * ROW_COLS // 2, (part + 1) * ROW_COLS // 2) for part in range(2)]
            if TAIL == 4:
                differences(last)
                for cols in halves:
                    accumulate(rt, SIDE - 1, False, cols)
                for cols in halves:
                    for p in (1, 2, 3, 0):
                        pixel_row(rt, p, cols)
                return
            for part in range(2):
                cols = halves[part]
                differences(last, (part,))
                accumulate(rt, SIDE - 1, False, cols)
                for p in (1, 2, 3, 0):
                    pixel_row(rt, p, cols)
